import numpy as np
import ml_dtypes


def mxq(x, axis, fmt="e4m3"):
    dtype, down = {"e4m3": (ml_dtypes.float8_e4m3fn, 7), "e5m2": (ml_dtypes.float8_e5m2, 14)}[fmt]
    v = np.moveaxis(np.asarray(x, np.float32).astype(ml_dtypes.bfloat16).astype(np.float64), axis, -1)
    blocks = v.reshape(v.shape[:-1] + (-1, 32))
    amax = np.abs(blocks).max(-1, keepdims=True)
    byte = np.maximum(np.where(amax > 0, np.frexp(amax)[1] - 1 + 127, 0) - down, 1)
    scale = np.exp2(byte - 127.0)
    codes = (blocks / scale).astype(np.float32).astype(dtype).astype(np.float64)
    return np.moveaxis((codes * scale).reshape(v.shape), -1, axis)


WIDE = False


def mx_kscale(k):
    if not WIDE:
        return np.ones(k)
    levels = np.array([10, -10, 5, -5, 0])
    a = np.random.permutation(np.resize(levels, k // 512 * 4)).reshape(k // 512, 4)
    idx = np.arange(k)
    return np.exp2(a[idx // 512, idx % 128 // 32])


BF16 = ml_dtypes.bfloat16


def bf(x):
    return np.asarray(x, np.float32).astype(BF16)


def f64(x):
    return np.asarray(x).astype(np.float64)


E2M1 = np.array([0.0, 0.5, 1.0, 1.5, 2.0, 3.0, 4.0, 6.0, -0.0, -0.5, -1.0, -1.5, -2.0, -3.0, -4.0, -6.0])


def pack_weight(w, fmt):
    k, n = w.shape
    w = f64(bf(w)).reshape(k // 32, 32, n)
    amax = np.abs(w).max(1)
    if fmt == "e4m3":
        byte = np.frexp(amax)[1] - 1 + 127 - 7
    else:
        mant, ex = np.frexp(amax / 6.0)
        byte = np.where(mant > 0.5, ex, ex - 1) + 127
    byte = np.clip(np.where(amax > 0, byte, 1), 1, 254)
    scaled = (w * np.exp2(127.0 - byte)[:, None, :]).reshape(k, n).astype(np.float32)
    by_word = np.ascontiguousarray(scaled.reshape(k // 512, 128, 4, n).transpose(0, 1, 3, 2))
    if fmt == "e4m3":
        words = by_word.astype(ml_dtypes.float8_e4m3fn).view(np.uint8)
    else:
        c = by_word.astype(ml_dtypes.float4_e2m1fn).view(np.uint8) & 0xF
        words = c[..., 0::2] | (c[..., 1::2] << 4)
    return np.ascontiguousarray(words), np.ascontiguousarray(byte.astype(np.uint8).reshape(k // 512, 16, n))


def unpack_weight(words, scales, fmt):
    g, p, n, _ = words.shape
    if fmt == "e4m3":
        vals = np.ascontiguousarray(words).view(ml_dtypes.float8_e4m3fn).astype(np.float64)
    else:
        nib = np.empty((g, p, n, 4), np.uint8)
        nib[..., 0::2] = words & 0xF
        nib[..., 1::2] = words >> 4
        vals = E2M1[nib]
    vals = vals * np.repeat(np.exp2(scales.astype(np.float64) - 127.0), 8, axis=1)[..., None]
    return vals.transpose(0, 1, 3, 2).reshape(g * 512, n)

def pack4(w):
    words, scales = pack_weight(w, "e2m1")
    return words.reshape(words.shape[0], 128, -1), scales


def unpack4(words, scales):
    return unpack_weight(words.reshape(words.shape[0], 128, -1, 2), scales, "e2m1")


B, IN, OUT = 512, 2048, 2048


def setup_inputs():
    s = mx_kscale(IN)
    input_data = bf(np.random.standard_normal((B, IN)) * s)
    weight_words, weight_scales = pack4((np.random.standard_normal((OUT, IN)) / np.sqrt(IN) / s).T)
    return {"input_data": input_data,
            "weight_words": weight_words,
            "weight_scales": weight_scales,
            "bias": bf(np.random.standard_normal(OUT) * 0.5),
            "prev_grad": bf(np.random.standard_normal((OUT, IN)) / np.sqrt(IN) / s),
            "prev_bias_grad": bf(np.random.standard_normal(OUT) * 0.5),
            "lr_samples": bf(np.random.uniform(0.1, 1.0, B))}


def reference(input_data, weight_words, weight_scales, bias, prev_grad, prev_bias_grad, lr_samples):
    xq = mxq(f64(input_data), 1, "e4m3")
    base = (xq @ unpack4(weight_words, weight_scales)) + f64(bias)
    pert = (xq @ mxq(f64(prev_grad), 1, "e4m3").T) + f64(prev_bias_grad)
    return base - f64(lr_samples)[:, None] * pert

@@ -1,0 +1,228 @@
+from contextlib import ExitStack
+
+import concourse.mybir as mybir
+from concourse.masks import make_identity
+
+F32 = mybir.dt.float32
+BF16 = mybir.dt.bfloat16
+I32 = mybir.dt.int32
+U32 = mybir.dt.uint32
+U8 = mybir.dt.uint8
+FP8X4 = mybir.dt.float8_e4m3fn_x4
+FP4X4 = mybir.dt.float4_e2m1fn_x4
+MULT = mybir.AluOpType.mult
+ADD = mybir.AluOpType.add
+
+P = 128
+B, IN, OUT = 512, 2048, 2048
+G = IN // 512
+MT = B // P
+NPAIR = OUT // 256
+NCH = OUT // 512
+FLOPS = 2 * 2 * B * IN * OUT
+
+
+def tile_optimizedlinear_kernel(
+    tc, input_data, weight_words, weight_scales, bias, prev_grad, prev_bias_grad, lr_samples, out
+):
+    nc = tc.nc
+    with ExitStack() as ctx:
+        keep = ctx.enter_context(tc.tile_pool(name="keep", bufs=1))
+        stage = ctx.enter_context(tc.tile_pool(name="stage", bufs=2))
+        pt = ctx.enter_context(tc.psum_pool(name="pt", bufs=4))
+        pp = ctx.enter_context(tc.psum_pool(name="pp", bufs=2))
+        pb = ctx.enter_context(tc.psum_pool(name="pb", bufs=2))
+        ctx.enter_context(tc.manual_schedule())
+
+        ident = keep.tile([P, P], F32, name="ident")
+        lr_rows = keep.tile([P, P], BF16, name="lr_rows")
+        lr_neg = keep.tile([P, P], F32, name="lr_neg")
+        nlr = keep.tile([P, MT], F32, name="nlr")
+        x_raw = [keep.tile([P, IN], BF16, name="x_raw%d" % m) for m in range(MT)]
+        g_raw = [keep.tile([P, IN], BF16, name="g_raw%d" % j) for j in range(OUT // P)]
+        w_words = [keep.tile([P, 2 * OUT], U8, name="w_words%d" % g, align_bytes=64) for g in range(G)]
+        w_planes = keep.tile([P, G, OUT], U8, name="w_planes", align_bytes=64)
+        xc = [keep.tile([P, G, P], U32, name="xc%d" % m, align_bytes=64) for m in range(MT)]
+        xs = [keep.tile([P, G, P], U8, name="xs%d" % m, align_bytes=64) for m in range(MT)]
+        gc = [keep.tile([P, G, 256], U32, name="gc%d" % h, align_bytes=64) for h in range(NPAIR)]
+        gs = [keep.tile([P, G, 256], U8, name="gs%d" % h, align_bytes=64) for h in range(NPAIR)]
+        bias_bc = keep.tile([P, OUT], BF16, name="bias_bc")
+        pbias_bc = keep.tile([P, OUT], BF16, name="pbias_bc")
+        o = [[keep.tile([P, 512], F32, name="o%d_%d" % (m, c)) for c in range(NCH)] for m in range(MT)]
+
+        make_identity(nc, ident[:])
+        nc.vector.memset(lr_rows[:], 0.0)
+        nc.vector.memset(w_planes[:].bitcast(I32), 0)
+        nc.scalar.dma_start(out=lr_rows[0:MT, :], in_=lr_samples.rearrange("(m p) -> m p", p=P))
+
+        def load_g(j):
+            nc.sync.dma_start(out=g_raw[j][:], in_=prev_grad[P * j:P * (j + 1), :])
+
+        for m in range(MT):
+            nc.sync.dma_start(out=x_raw[m][:], in_=input_data[P * m:P * (m + 1), :])
+        for j in range(0, 4):
+            load_g(j)
+        nc.sync.dma_start(out=pbias_bc[:], in_=prev_bias_grad.partition_broadcast(P))
+        nc.sync.dma_start(out=bias_bc[:], in_=bias.partition_broadcast(P))
+        for j in range(4, 8):
+            load_g(j)
+        scale_rows = weight_scales.rearrange("g q n -> q g n")
+        for b in range(2):
+            for r in range(4):
+                nc.sync.dma_start(
+                    out=w_planes[32 * b + r:P:64, :, :].bitcast(I32),
+                    in_=scale_rows[4 * b + r:16:8, :, :].bitcast(I32),
+                )
+        for g in range(G):
+            nc.sync.dma_start(out=w_words[g][:].bitcast(I32), in_=weight_words[g].bitcast(I32))
+        for j in range(8, 16):
+            load_g(j)
+
+        def lr_column():
+            nc.vector.tensor_scalar(out=lr_neg[:], in0=lr_rows[:], scalar1=-1.0, scalar2=None, op0=MULT)
+            lr_bank = pt.tile([P, 2, 2, P], F32, name="tbank")
+            nc.tensor.transpose(lr_bank[:, 0, 0, :], lr_neg[:], ident[:])
+            nc.vector.tensor_copy(out=nlr[:], in_=lr_bank[:, 0, 0, 0:MT])
+
+        def transpose_tile(src, dst_words, rows, engines):
+            src_words = src[:].bitcast(F32)
+            for gp in range(2):
+                tbank = pt.tile([P, 2, 2, P], F32, name="tbank")
+                for g2 in range(2):
+                    g = 2 * gp + g2
+                    for u in range(2):
+                        nc.tensor.transpose(tbank[:, g2, u, :], src_words[:, 256 * g + u:256 * (g + 1):2], ident[:])
+                dst = dst_words[:, 2 * gp:2 * gp + 2, rows, :]
+                view = tbank[:].rearrange("p g u r -> p g r u")
+                if engines[gp] == "v":
+                    nc.vector.tensor_copy(out=dst, in_=view)
+                else:
+                    nc.scalar.copy(out=dst, in_=view)
+
+        xg = {}
+
+        def tx(m):
+            xg[m] = stage.tile([P, G, P, 4], BF16, name="xg", align_bytes=64)
+            transpose_tile(x_raw[m], xg[m][:].bitcast(F32), slice(0, P), "sv")
+
+        def qx(m):
+            nc.vector.quantize_mx(
+                out=xc[m][:].rearrange("p g r -> p (g r)").bitcast(FP8X4),
+                scales=xs[m][:].rearrange("p g r -> p (g r)"),
+                in_=xg[m][:].rearrange("p g r t -> p (g r t)"),
+            )
+
+        gg = {}
+
+        def tg(h):
+            gg[h] = stage.tile([P, G, 256, 4], BF16, name="gg", align_bytes=64)
+            for jj in range(2):
+                transpose_tile(g_raw[2 * h + jj], gg[h][:].bitcast(F32), slice(P * jj, P * (jj + 1)), "ss")
+
+        def qg(h):
+            for a in range(2):
+                nc.vector.quantize_mx(
+                    out=gc[h][:, 2 * a:2 * a + 2, :].rearrange("p g r -> p (g r)").bitcast(FP8X4),
+                    scales=gs[h][:, 2 * a:2 * a + 2, :].rearrange("p g r -> p (g r)"),
+                    in_=gg[h][:, 2 * a:2 * a + 2, :, :].rearrange("p g r t -> p (g r t)"),
+                )
+
+        def ct(c, m):
+            cols = slice(512 * c, 512 * (c + 1))
+            nc.vector.scalar_tensor_tensor(
+                out=o[m][c][:], in0=pbias_bc[:, cols], scalar=nlr[:, m:m + 1], in1=bias_bc[:, cols], op0=MULT, op1=ADD
+            )
+
+        def pert(h):
+            c, half = h // 2, h % 2
+            for mp in range(2):
+                pbank = pp.tile([P, 2, 256], F32, name="pbank")
+                for i in range(2):
+                    m = 2 * mp + i
+                    for g in range(G):
+                        nc.tensor.matmul_mx(
+                            out=pbank[:, i, :],
+                            lhsT=xc[m][:, g, :].bitcast(FP8X4),
+                            lhsT_scale=xs[m][:, g, :],
+                            rhs=gc[h][:, g, :].bitcast(FP8X4),
+                            rhs_scale=gs[h][:, g, :],
+                            start=(g == 0),
+                            stop=(g == G - 1),
+                        )
+                for i in range(2):
+                    m = 2 * mp + i
+                    dst = o[m][c][:, 256 * half:256 * (half + 1)]
+                    nc.vector.scalar_tensor_tensor(
+                        out=dst, in0=pbank[:, i, :], scalar=nlr[:, m:m + 1], in1=dst, op0=MULT, op1=ADD
+                    )
+
+        def base(c, m):
+            bbank = pb.tile([P, 512], F32, name="bbank")
+            for g in range(G):
+                nc.tensor.matmul_mx(
+                    out=bbank[:],
+                    lhsT=xc[m][:, g, :].bitcast(FP8X4),
+                    lhsT_scale=xs[m][:, g, :],
+                    rhs=w_words[g][:, 1024 * c:1024 * (c + 1)].bitcast(FP4X4),
+                    rhs_scale=w_planes[:, g, 512 * c:512 * (c + 1)],
+                    start=(g == 0),
+                    stop=(g == G - 1),
+                )
+            nc.vector.tensor_tensor(out=o[m][c][:], in0=bbank[:], in1=o[m][c][:], op=ADD)
+            nc.sync.dma_start(out=out[P * m:P * (m + 1), 512 * c:512 * (c + 1)], in_=o[m][c][:])
+
+        def cts(c):
+            for m in range(MT):
+                ct(c, m)
+
+        tx(0)
+        tx(1)
+        qx(0)
+        tx(2)
+        qx(1)
+        tx(3)
+        qx(2)
+        lr_column()
+        tg(0)
+        qx(3)
+        qg(0)
+        tg(1)
+        qg(1)
+        cts(0)
+        pert(0)
+        tg(2)
+        qg(2)
+        pert(1)
+        tg(3)
+        cts(1)
+        qg(3)
+        pert(2)
+        pert(3)
+        base(0, 0)
+        base(0, 1)
+        tg(4)
+        cts(2)
+        qg(4)
+        base(0, 2)
+        base(0, 3)
+        tg(5)
+        qg(5)
+        pert(4)
+        base(1, 0)
+        base(1, 1)
+        tg(6)
+        cts(3)
+        qg(6)
+        pert(5)
+        base(1, 2)
+        base(1, 3)
+        tg(7)
+        qg(7)
+        pert(6)
+        base(2, 0)
+        base(2, 1)
+        pert(7)
+        base(2, 2)
+        base(2, 3)
+        for m in range(MT):
+            base(3, m)

@@ -28,6 +28,8 @@ def tile_optimizedlinear_kernel(
     nc = tc.nc
     with ExitStack() as ctx:
         keep = ctx.enter_context(tc.tile_pool(name="keep", bufs=1))
+        rawp = ctx.enter_context(tc.tile_pool(name="rawp", bufs=12))
+        sortp = ctx.enter_context(tc.tile_pool(name="sortp", bufs=6))
         stage = ctx.enter_context(tc.tile_pool(name="stage", bufs=2))
         pt = ctx.enter_context(tc.psum_pool(name="pt", bufs=4))
         pp = ctx.enter_context(tc.psum_pool(name="pp", bufs=2))
@@ -38,8 +40,6 @@ def tile_optimizedlinear_kernel(
         lr_rows = keep.tile([P, P], BF16, name="lr_rows")
         lr_neg = keep.tile([P, P], F32, name="lr_neg")
         nlr = keep.tile([P, MT], F32, name="nlr")
-        x_raw = [keep.tile([P, IN], BF16, name="x_raw%d" % m) for m in range(MT)]
-        g_raw = [keep.tile([P, IN], BF16, name="g_raw%d" % j) for j in range(OUT // P)]
         w_words = [keep.tile([P, 2 * OUT], U8, name="w_words%d" % g, align_bytes=64) for g in range(G)]
         w_planes = keep.tile([P, G, OUT], U8, name="w_planes", align_bytes=64)
         xc = [keep.tile([P, G, P], U32, name="xc%d" % m, align_bytes=64) for m in range(MT)]
@@ -55,11 +55,19 @@ def tile_optimizedlinear_kernel(
         nc.vector.memset(w_planes[:].bitcast(I32), 0)
         nc.scalar.dma_start(out=lr_rows[0:MT, :], in_=lr_samples.rearrange("(m p) -> m p", p=P))
 
+        x_raw = {}
+        g_raw = {}
+
+        def load_x(m):
+            x_raw[m] = rawp.tile([P, IN], BF16, name="raw")
+            nc.sync.dma_start(out=x_raw[m][:], in_=input_data[P * m:P * (m + 1), :])
+
         def load_g(j):
+            g_raw[j] = rawp.tile([P, IN], BF16, name="raw")
             nc.sync.dma_start(out=g_raw[j][:], in_=prev_grad[P * j:P * (j + 1), :])
 
         for m in range(MT):
-            nc.sync.dma_start(out=x_raw[m][:], in_=input_data[P * m:P * (m + 1), :])
+            load_x(m)
         for j in range(0, 4):
             load_g(j)
         nc.sync.dma_start(out=pbias_bc[:], in_=prev_bias_grad.partition_broadcast(P))
@@ -75,8 +83,6 @@ def tile_optimizedlinear_kernel(
                 )
         for g in range(G):
             nc.sync.dma_start(out=w_words[g][:].bitcast(I32), in_=weight_words[g].bitcast(I32))
-        for j in range(8, 16):
-            load_g(j)
 
         def lr_column():
             nc.vector.tensor_scalar(out=lr_neg[:], in0=lr_rows[:], scalar1=-1.0, scalar2=None, op0=MULT)
@@ -84,26 +90,40 @@ def tile_optimizedlinear_kernel(
             nc.tensor.transpose(lr_bank[:, 0, 0, :], lr_neg[:], ident[:])
             nc.vector.tensor_copy(out=nlr[:], in_=lr_bank[:, 0, 0, 0:MT])
 
-        def transpose_tile(src, dst_words, rows, engines):
-            src_words = src[:].bitcast(F32)
+        def sort_words(src, engine):
+            srt = sortp.tile([P, G, 2, P], F32, name="srt")
+            view = src[:].bitcast(F32).rearrange("r (g p u) -> r g u p", g=G, u=2)
+            if engine == "v":
+                nc.vector.tensor_copy(out=srt[:], in_=view)
+            else:
+                nc.scalar.copy(out=srt[:], in_=view)
+            return srt
+
+        def transpose_tile(srt, dst_words, rows):
             for gp in range(2):
                 tbank = pt.tile([P, 2, 2, P], F32, name="tbank")
                 for g2 in range(2):
-                    g = 2 * gp + g2
                     for u in range(2):
-                        nc.tensor.transpose(tbank[:, g2, u, :], src_words[:, 256 * g + u:256 * (g + 1):2], ident[:])
-                dst = dst_words[:, 2 * gp:2 * gp + 2, rows, :]
-                view = tbank[:].rearrange("p g u r -> p g r u")
-                if engines[gp] == "v":
-                    nc.vector.tensor_copy(out=dst, in_=view)
-                else:
-                    nc.scalar.copy(out=dst, in_=view)
+                        nc.tensor.transpose(tbank[:, g2, u, :], srt[:, 2 * gp + g2, u, :], ident[:])
+                nc.scalar.copy(
+                    out=dst_words[:, 2 * gp:2 * gp + 2, rows, :], in_=tbank[:].rearrange("p g u r -> p g r u")
+                )
 
+        x_srt = {}
+        g_srt = {}
         xg = {}
+        gg = {}
+
+        def sx(m, engine):
+            x_srt[m] = sort_words(x_raw[m], engine)
+
+        def sg(h, engine):
+            for j in (2 * h, 2 * h + 1):
+                g_srt[j] = sort_words(g_raw[j], engine)
 
         def tx(m):
             xg[m] = stage.tile([P, G, P, 4], BF16, name="xg", align_bytes=64)
-            transpose_tile(x_raw[m], xg[m][:].bitcast(F32), slice(0, P), "sv")
+            transpose_tile(x_srt[m], xg[m][:].bitcast(F32), slice(0, P))
 
         def qx(m):
             nc.vector.quantize_mx(
@@ -112,12 +132,10 @@ def tile_optimizedlinear_kernel(
                 in_=xg[m][:].rearrange("p g r t -> p (g r t)"),
             )
 
-        gg = {}
-
         def tg(h):
             gg[h] = stage.tile([P, G, 256, 4], BF16, name="gg", align_bytes=64)
             for jj in range(2):
-                transpose_tile(g_raw[2 * h + jj], gg[h][:].bitcast(F32), slice(P * jj, P * (jj + 1)), "ss")
+                transpose_tile(g_srt[2 * h + jj], gg[h][:].bitcast(F32), slice(P * jj, P * (jj + 1)))
 
         def qg(h):
             for a in range(2):
@@ -127,11 +145,13 @@ def tile_optimizedlinear_kernel(
                     in_=gg[h][:, 2 * a:2 * a + 2, :, :].rearrange("p g r t -> p (g r t)"),
                 )
 
-        def ct(c, m):
+        def cts(c):
             cols = slice(512 * c, 512 * (c + 1))
-            nc.vector.scalar_tensor_tensor(
-                out=o[m][c][:], in0=pbias_bc[:, cols], scalar=nlr[:, m:m + 1], in1=bias_bc[:, cols], op0=MULT, op1=ADD
-            )
+            for m in range(MT):
+                nc.vector.scalar_tensor_tensor(
+                    out=o[m][c][:], in0=pbias_bc[:, cols], scalar=nlr[:, m:m + 1], in1=bias_bc[:, cols],
+                    op0=MULT, op1=ADD,
+                )
 
         def pert(h):
             c, half = h // 2, h % 2
@@ -171,41 +191,57 @@ def tile_optimizedlinear_kernel(
             nc.vector.tensor_tensor(out=o[m][c][:], in0=bbank[:], in1=o[m][c][:], op=ADD)
             nc.sync.dma_start(out=out[P * m:P * (m + 1), 512 * c:512 * (c + 1)], in_=o[m][c][:])
 
-        def cts(c):
-            for m in range(MT):
-                ct(c, m)
-
+        sx(0, "v")
+        load_g(8)
         tx(0)
+        sx(1, "v")
+        load_g(9)
         tx(1)
         qx(0)
+        sx(2, "v")
+        load_g(10)
         tx(2)
         qx(1)
+        sx(3, "v")
+        load_g(11)
         tx(3)
         qx(2)
         lr_column()
+        sg(0, "v")
+        load_g(12)
+        load_g(13)
         tg(0)
         qx(3)
-        qg(0)
+        sg(1, "v")
+        load_g(14)
+        load_g(15)
         tg(1)
+        qg(0)
+        sg(2, "s")
         qg(1)
         cts(0)
         pert(0)
         tg(2)
+        sg(3, "s")
         qg(2)
         pert(1)
         tg(3)
+        sg(4, "s")
         cts(1)
         qg(3)
         pert(2)
+        sg(5, "s")
         pert(3)
         base(0, 0)
         base(0, 1)
         tg(4)
+        sg(6, "s")
         cts(2)
         qg(4)
         base(0, 2)
         base(0, 3)
         tg(5)
+        sg(7, "s")
         qg(5)
         pert(4)
         base(1, 0)

@@ -21,6 +21,36 @@ NPAIR = OUT // 256
 NCH = OUT // 512
 FLOPS = 2 * 2 * B * IN * OUT
 
+PLAN = (
+    ("setup",), ("sort", "x1", "n"), ("sort", "x0", "n"), ("spread", 2, "s", "s"), ("loadx", 3), ("sort", "x2", "n"),
+    ("loadx", 0), ("lrneg",), ("spread", 0, "v", "v"), ("selneg",), ("loadx", 1), ("lrT",),
+    ("loadx", 2), ("loadg", 1), ("loadsc", 0, 1), ("ct", 2, 2, "v"), ("tt", "x0", "s", "s"), ("qx", 0),
+    ("loadg", 0), ("loadwc", 0), ("loadg", 3), ("tt", "x1", "s", "v"), ("qx", 1), ("loadwc", 1),
+    ("loadg", 2), ("loadsc", 1, 4), ("sort", "g1", "n"), ("sort", "g0", "n"), ("loadg", 5), ("sort", "g6", "n"),
+    ("spread", 1, "s", "s"), ("sort", "x3", "n"), ("loadg", 4), ("loadg", 6), ("ct", 1, 3, "v"), ("ct", 0, 0, "v"),
+    ("tt", "x3", "s", "s"), ("tt", "x2", "s", "s"), ("ct", 1, 0, "v"), ("qx", 3), ("tt", "g1", "s", "s"), ("loadwc", 2),
+    ("qx", 2), ("ct", 0, 1, "v"), ("sort", "g3", "s"), ("ct", 0, 2, "v"), ("spread", 3, "v", "s"), ("cpe", 0, 3, "s"),
+    ("tt", "g0", "s", "v"), ("sort", "g2", "s"), ("ct", 3, 3, "v"), ("base", 0, 0), ("loadwc", 3), ("base", 0, 3),
+    ("ct", 1, 2, "v"), ("base", 0, 1), ("loadg", 9), ("loadg", 10), ("qg", 0, 1), ("cpe", 2, 1, "s"),
+    ("base", 0, 2), ("loadg", 8), ("tt", "g3", "s", "s"), ("ct", 2, 0, "v"), ("tt", "g2", "s", "s"), ("qg", 0, 0),
+    ("sort", "g5", "v"), ("loadg", 7), ("sort", "g4", "s"), ("ct", 1, 1, "v"), ("base", 1, 1), ("base", 1, 2),
+    ("qg", 1, 0), ("base", 1, 3), ("qg", 1, 1), ("loadg", 14), ("pert", 0, 1), ("tt", "g4", "s", "v"),
+    ("tt", "g5", "s", "s"), ("pert", 1, 0), ("ct", 2, 3, "v"), ("base", 2, 0), ("qg", 2, 0), ("ct", 3, 0, "v"),
+    ("pert", 0, 0), ("ct", 3, 2, "v"), ("loadg", 11), ("sort", "g8", "s"), ("sort", "g9", "s"), ("ct", 3, 1, "v"),
+    ("base", 1, 0), ("pert", 1, 1), ("sort", "g10", "s"), ("base", 2, 3), ("qg", 2, 1), ("base", 2, 2),
+    ("loadg", 15), ("base", 2, 1), ("sort", "g7", "s"), ("loadg", 13), ("base", 3, 0), ("loadg", 12),
+    ("tt", "g9", "s", "s"), ("tt", "g6", "v", "s"), ("tt", "g7", "v", "s"), ("qg", 3, 0), ("sort", "g11", "s"), ("sort", "g12", "s"),
+    ("tt", "g8", "v", "v"), ("base", 3, 1), ("qg", 4, 0), ("qg", 3, 1), ("qg", 4, 1), ("base", 3, 2),
+    ("pert", 2, 1), ("tt", "g11", "v", "s"), ("tt", "g10", "s", "s"), ("pert", 2, 0), ("sort", "g13", "s"), ("pert", 3, 0),
+    ("pert", 3, 1), ("qg", 5, 0), ("store", 0, 3), ("tt", "g13", "s", "s"), ("sort", "g15", "s"), ("tt", "g12", "v", "s"),
+    ("store", 1, 1), ("sort", "g14", "s"), ("store", 1, 3), ("store", 0, 2), ("qg", 6, 0), ("qg", 5, 1),
+    ("pert", 4, 1), ("store", 1, 2), ("qg", 6, 1), ("base", 3, 3), ("store", 1, 0), ("pert", 5, 1),
+    ("pert", 5, 0), ("tt", "g15", "s", "v"), ("store", 0, 1), ("tt", "g14", "v", "s"), ("qg", 7, 1), ("qg", 7, 0),
+    ("store", 2, 2), ("pert", 4, 0), ("pert", 6, 0), ("store", 2, 3), ("store", 2, 1), ("pert", 6, 1),
+    ("store", 0, 0), ("pert", 7, 1), ("store", 2, 0), ("pert", 7, 0), ("store", 3, 2), ("store", 3, 3),
+    ("store", 3, 0), ("store", 3, 1),
+)
+
 
 def tile_optimizedlinear_kernel(
     tc, input_data, weight_words, weight_scales, bias, prev_grad, prev_bias_grad, lr_samples, out
@@ -32,16 +62,17 @@ def tile_optimizedlinear_kernel(
         sortp = ctx.enter_context(tc.tile_pool(name="sortp", bufs=6))
         stage = ctx.enter_context(tc.tile_pool(name="stage", bufs=2))
         pt = ctx.enter_context(tc.psum_pool(name="pt", bufs=4))
-        pp = ctx.enter_context(tc.psum_pool(name="pp", bufs=2))
-        pb = ctx.enter_context(tc.psum_pool(name="pb", bufs=2))
+        pa = ctx.enter_context(tc.psum_pool(name="pa", bufs=4))
         ctx.enter_context(tc.manual_schedule())
 
         ident = keep.tile([P, P], F32, name="ident")
         lr_rows = keep.tile([P, P], BF16, name="lr_rows")
         lr_neg = keep.tile([P, P], F32, name="lr_neg")
         nlr = keep.tile([P, MT], F32, name="nlr")
-        w_words = [keep.tile([P, 2 * OUT], U8, name="w_words%d" % g, align_bytes=64) for g in range(G)]
-        w_planes = keep.tile([P, G, OUT], U8, name="w_planes", align_bytes=64)
+        b_rows = keep.tile([P, OUT], BF16, name="b_rows")
+        pick = [keep.tile([P, P], BF16, name="pick%d" % i) for i in range(2)]
+        sel = keep.tile([P, B], BF16, name="sel")
+        w_words = [keep.tile([P, G, 1024], U8, name="w_words%d" % c, align_bytes=64) for c in range(NCH)]
         xc = [keep.tile([P, G, P], U32, name="xc%d" % m, align_bytes=64) for m in range(MT)]
         xs = [keep.tile([P, G, P], U8, name="xs%d" % m, align_bytes=64) for m in range(MT)]
         gc = [keep.tile([P, G, 256], U32, name="gc%d" % h, align_bytes=64) for h in range(NPAIR)]
@@ -49,81 +80,97 @@ def tile_optimizedlinear_kernel(
         bias_bc = keep.tile([P, OUT], BF16, name="bias_bc")
         pbias_bc = keep.tile([P, OUT], BF16, name="pbias_bc")
         o = [[keep.tile([P, 512], F32, name="o%d_%d" % (m, c)) for c in range(NCH)] for m in range(MT)]
-
-        make_identity(nc, ident[:])
-        nc.vector.memset(lr_rows[:], 0.0)
-        nc.vector.memset(w_planes[:].bitcast(I32), 0)
-        nc.scalar.dma_start(out=lr_rows[0:MT, :], in_=lr_samples.rearrange("(m p) -> m p", p=P))
-
-        x_raw = {}
-        g_raw = {}
-
-        def load_x(m):
-            x_raw[m] = rawp.tile([P, IN], BF16, name="raw")
-            nc.sync.dma_start(out=x_raw[m][:], in_=input_data[P * m:P * (m + 1), :])
-
-        def load_g(j):
-            g_raw[j] = rawp.tile([P, IN], BF16, name="raw")
-            nc.sync.dma_start(out=g_raw[j][:], in_=prev_grad[P * j:P * (j + 1), :])
-
-        for m in range(MT):
-            load_x(m)
-        for j in range(0, 4):
-            load_g(j)
-        nc.sync.dma_start(out=pbias_bc[:], in_=prev_bias_grad.partition_broadcast(P))
-        nc.sync.dma_start(out=bias_bc[:], in_=bias.partition_broadcast(P))
-        for j in range(4, 8):
-            load_g(j)
+        planes = {}
+        plane_of = {}
+        for tk in PLAN:
+            if tk[0] == "loadsc":
+                planes[tk[1]] = keep.tile([P, G, 512 * (tk[2] - tk[1])], U8, name="planes%d" % tk[1], align_bytes=64)
+                for c in range(tk[1], tk[2]):
+                    plane_of[c] = (planes[tk[1]], 512 * (c - tk[1]))
         scale_rows = weight_scales.rearrange("g q n -> q g n")
-        for b in range(2):
+        raw = {}
+        srt = {}
+        xg = {}
+        gg = {}
+
+        def evac(engine, dst, src):
+            if engine == "v":
+                nc.vector.tensor_copy(out=dst, in_=src)
+            else:
+                nc.scalar.copy(out=dst, in_=src)
+
+        def setup():
+            make_identity(nc, ident[:])
+            nc.vector.memset(b_rows[:].bitcast(I32), 0)
+            nc.scalar.dma_start(out=b_rows[0:1, :], in_=bias.unsqueeze(0))
+            nc.scalar.dma_start(out=b_rows[32:33, :], in_=prev_bias_grad.unsqueeze(0))
+            nc.vector.memset(lr_rows[:], 0.0)
+            nc.scalar.dma_start(out=lr_rows[0:MT, :], in_=lr_samples.rearrange("(m p) -> m p", p=P))
+            for i in range(2):
+                nc.vector.memset(pick[i][:], 0.0)
+                nc.vector.memset(pick[i][32 * i:32 * i + 1, :], 1.0)
+            nc.vector.memset(sel[:], 0.0)
+            nc.vector.memset(sel[0:1, :], 1.0)
+            nc.scalar.dma_start(out=sel[32:33, :], in_=lr_samples.unsqueeze(0))
+            for a in sorted(planes):
+                nc.vector.memset(planes[a][:].bitcast(I32), 0)
+
+        def load_raw(key, rows):
+            raw[key] = rawp.tile([P, IN], BF16, name="raw")
+            nc.sync.dma_start(out=raw[key][:], in_=rows)
+
+        def loadwc(c):
+            nc.sync.dma_start(
+                out=w_words[c][:].bitcast(I32),
+                in_=weight_words[:, :, 1024 * c:1024 * (c + 1)].rearrange("g p b -> p g b").bitcast(I32),
+            )
+
+        def loadsc(a, b):
             for r in range(4):
                 nc.sync.dma_start(
-                    out=w_planes[32 * b + r:P:64, :, :].bitcast(I32),
-                    in_=scale_rows[4 * b + r:16:8, :, :].bitcast(I32),
+                    out=planes[a][r:P:32, :, :].bitcast(I32),
+                    in_=scale_rows[r:16:4, :, 512 * a:512 * b].bitcast(I32),
                 )
-        for g in range(G):
-            nc.sync.dma_start(out=w_words[g][:].bitcast(I32), in_=weight_words[g].bitcast(I32))
 
-        def lr_column():
+        def lrneg():
             nc.vector.tensor_scalar(out=lr_neg[:], in0=lr_rows[:], scalar1=-1.0, scalar2=None, op0=MULT)
+
+        def selneg():
+            nc.vector.tensor_scalar(out=sel[32:33, :], in0=sel[32:33, :], scalar1=-1.0, scalar2=None, op0=MULT)
+
+        def lr_t():
             lr_bank = pt.tile([P, 2, 2, P], F32, name="tbank")
             nc.tensor.transpose(lr_bank[:, 0, 0, :], lr_neg[:], ident[:])
             nc.vector.tensor_copy(out=nlr[:], in_=lr_bank[:, 0, 0, 0:MT])
 
-        def sort_words(src, engine):
-            srt = sortp.tile([P, G, 2, P], F32, name="srt")
-            view = src[:].bitcast(F32).rearrange("r (g p u) -> r g u p", g=G, u=2)
-            if engine == "v":
-                nc.vector.tensor_copy(out=srt[:], in_=view)
-            else:
-                nc.scalar.copy(out=srt[:], in_=view)
-            return srt
+        def word_view(key):
+            return raw[key][:].bitcast(F32).rearrange("r (g p u) -> r g u p", g=G, u=2)
 
-        def transpose_tile(srt, dst_words, rows):
+        def sort_words(key, engine):
+            if engine != "n":
+                sorted_words = sortp.tile([P, G, 2, P], F32, name="srt")
+                evac(engine, sorted_words[:], word_view(key))
+                srt[key] = sorted_words
+
+        def transposes(key, e0, e1):
+            idx = int(key[1:])
+            if key[0] == "x":
+                xg[idx] = stage.tile([P, G, P, 4], BF16, name="xg", align_bytes=64)
+                dst_words = xg[idx][:].bitcast(F32)
+                rows = slice(0, P)
+            else:
+                h = idx // 2
+                if h not in gg:
+                    gg[h] = stage.tile([P, G, 256, 4], BF16, name="gg", align_bytes=64)
+                dst_words = gg[h][:].bitcast(F32)
+                rows = slice(P * (idx % 2), P * (idx % 2 + 1))
+            words = srt[key] if key in srt else word_view(key)
             for gp in range(2):
                 tbank = pt.tile([P, 2, 2, P], F32, name="tbank")
                 for g2 in range(2):
                     for u in range(2):
-                        nc.tensor.transpose(tbank[:, g2, u, :], srt[:, 2 * gp + g2, u, :], ident[:])
-                nc.scalar.copy(
-                    out=dst_words[:, 2 * gp:2 * gp + 2, rows, :], in_=tbank[:].rearrange("p g u r -> p g r u")
-                )
-
-        x_srt = {}
-        g_srt = {}
-        xg = {}
-        gg = {}
-
-        def sx(m, engine):
-            x_srt[m] = sort_words(x_raw[m], engine)
-
-        def sg(h, engine):
-            for j in (2 * h, 2 * h + 1):
-                g_srt[j] = sort_words(g_raw[j], engine)
-
-        def tx(m):
-            xg[m] = stage.tile([P, G, P, 4], BF16, name="xg", align_bytes=64)
-            transpose_tile(x_srt[m], xg[m][:].bitcast(F32), slice(0, P))
+                        nc.tensor.transpose(tbank[:, g2, u, :], words[:, 2 * gp + g2, u, :], ident[:])
+                evac((e0, e1)[gp], dst_words[:, 2 * gp:2 * gp + 2, rows, :], tbank[:].rearrange("p g u r -> p g r u"))
 
         def qx(m):
             nc.vector.quantize_mx(
@@ -132,133 +179,110 @@ def tile_optimizedlinear_kernel(
                 in_=xg[m][:].rearrange("p g r t -> p (g r t)"),
             )
 
-        def tg(h):
-            gg[h] = stage.tile([P, G, 256, 4], BF16, name="gg", align_bytes=64)
-            for jj in range(2):
-                transpose_tile(g_srt[2 * h + jj], gg[h][:].bitcast(F32), slice(P * jj, P * (jj + 1)))
+        def qg(h, a):
+            nc.vector.quantize_mx(
+                out=gc[h][:, 2 * a:2 * a + 2, :].rearrange("p g r -> p (g r)").bitcast(FP8X4),
+                scales=gs[h][:, 2 * a:2 * a + 2, :].rearrange("p g r -> p (g r)"),
+                in_=gg[h][:, 2 * a:2 * a + 2, :, :].rearrange("p g r t -> p (g r t)"),
+            )
 
-        def qg(h):
-            for a in range(2):
-                nc.vector.quantize_mx(
-                    out=gc[h][:, 2 * a:2 * a + 2, :].rearrange("p g r -> p (g r)").bitcast(FP8X4),
-                    scales=gs[h][:, 2 * a:2 * a + 2, :].rearrange("p g r -> p (g r)"),
-                    in_=gg[h][:, 2 * a:2 * a + 2, :, :].rearrange("p g r t -> p (g r t)"),
-                )
-
-        def cts(c):
+        def spread(c, e0, e1):
             cols = slice(512 * c, 512 * (c + 1))
-            for m in range(MT):
-                nc.vector.scalar_tensor_tensor(
-                    out=o[m][c][:], in0=pbias_bc[:, cols], scalar=nlr[:, m:m + 1], in1=bias_bc[:, cols],
-                    op0=MULT, op1=ADD,
-                )
+            for i in range(2):
+                bank = pa.tile([P, 512], F32, name="acc")
+                nc.tensor.matmul(out=bank[:], lhsT=pick[i][:], rhs=b_rows[:, cols], start=True, stop=True)
+                evac((e0, e1)[i], (bias_bc, pbias_bc)[i][:, cols], bank[:])
 
-        def pert(h):
+        def ct(c, m):
+            cols = slice(512 * c, 512 * (c + 1))
+            nc.vector.scalar_tensor_tensor(
+                out=o[m][c][:], in0=pbias_bc[:, cols], scalar=nlr[:, m:m + 1], in1=bias_bc[:, cols], op0=MULT, op1=ADD
+            )
+
+        def cpe(c, m, engine):
+            bank = pa.tile([P, 512], F32, name="acc")
+            nc.tensor.matmul(
+                out=bank[:], lhsT=sel[:, P * m:P * (m + 1)], rhs=b_rows[:, 512 * c:512 * (c + 1)], start=True, stop=True
+            )
+            evac(engine, o[m][c][:], bank[:])
+
+        def pert(h, mp):
             c, half = h // 2, h % 2
-            for mp in range(2):
-                pbank = pp.tile([P, 2, 256], F32, name="pbank")
-                for i in range(2):
-                    m = 2 * mp + i
-                    for g in range(G):
-                        nc.tensor.matmul_mx(
-                            out=pbank[:, i, :],
-                            lhsT=xc[m][:, g, :].bitcast(FP8X4),
-                            lhsT_scale=xs[m][:, g, :],
-                            rhs=gc[h][:, g, :].bitcast(FP8X4),
-                            rhs_scale=gs[h][:, g, :],
-                            start=(g == 0),
-                            stop=(g == G - 1),
-                        )
-                for i in range(2):
-                    m = 2 * mp + i
-                    dst = o[m][c][:, 256 * half:256 * (half + 1)]
-                    nc.vector.scalar_tensor_tensor(
-                        out=dst, in0=pbank[:, i, :], scalar=nlr[:, m:m + 1], in1=dst, op0=MULT, op1=ADD
+            bank = pa.tile([P, 512], F32, name="acc")
+            for i in range(2):
+                m = 2 * mp + i
+                for g in range(G):
+                    nc.tensor.matmul_mx(
+                        out=bank[:, 256 * i:256 * (i + 1)],
+                        lhsT=xc[m][:, g, :].bitcast(FP8X4),
+                        lhsT_scale=xs[m][:, g, :],
+                        rhs=gc[h][:, g, :].bitcast(FP8X4),
+                        rhs_scale=gs[h][:, g, :],
+                        start=(g == 0),
+                        stop=(g == G - 1),
                     )
+            for i in range(2):
+                m = 2 * mp + i
+                dst = o[m][c][:, 256 * half:256 * (half + 1)]
+                nc.vector.scalar_tensor_tensor(
+                    out=dst, in0=bank[:, 256 * i:256 * (i + 1)], scalar=nlr[:, m:m + 1], in1=dst, op0=MULT, op1=ADD
+                )
 
         def base(c, m):
-            bbank = pb.tile([P, 512], F32, name="bbank")
+            bank = pa.tile([P, 512], F32, name="acc")
+            plane, off = plane_of[c]
             for g in range(G):
                 nc.tensor.matmul_mx(
-                    out=bbank[:],
+                    out=bank[:],
                     lhsT=xc[m][:, g, :].bitcast(FP8X4),
                     lhsT_scale=xs[m][:, g, :],
-                    rhs=w_words[g][:, 1024 * c:1024 * (c + 1)].bitcast(FP4X4),
-                    rhs_scale=w_planes[:, g, 512 * c:512 * (c + 1)],
+                    rhs=w_words[c][:, g, :].bitcast(FP4X4),
+                    rhs_scale=plane[:, g, off:off + 512],
                     start=(g == 0),
                     stop=(g == G - 1),
                 )
-            nc.vector.tensor_tensor(out=o[m][c][:], in0=bbank[:], in1=o[m][c][:], op=ADD)
+            nc.vector.tensor_tensor(out=o[m][c][:], in0=bank[:], in1=o[m][c][:], op=ADD)
+
+        def store(c, m):
             nc.sync.dma_start(out=out[P * m:P * (m + 1), 512 * c:512 * (c + 1)], in_=o[m][c][:])
 
-        sx(0, "v")
-        load_g(8)
-        tx(0)
-        sx(1, "v")
-        load_g(9)
-        tx(1)
-        qx(0)
-        sx(2, "v")
-        load_g(10)
-        tx(2)
-        qx(1)
-        sx(3, "v")
-        load_g(11)
-        tx(3)
-        qx(2)
-        lr_column()
-        sg(0, "v")
-        load_g(12)
-        load_g(13)
-        tg(0)
-        qx(3)
-        sg(1, "v")
-        load_g(14)
-        load_g(15)
-        tg(1)
-        qg(0)
-        sg(2, "s")
-        qg(1)
-        cts(0)
-        pert(0)
-        tg(2)
-        sg(3, "s")
-        qg(2)
-        pert(1)
-        tg(3)
-        sg(4, "s")
-        cts(1)
-        qg(3)
-        pert(2)
-        sg(5, "s")
-        pert(3)
-        base(0, 0)
-        base(0, 1)
-        tg(4)
-        sg(6, "s")
-        cts(2)
-        qg(4)
-        base(0, 2)
-        base(0, 3)
-        tg(5)
-        sg(7, "s")
-        qg(5)
-        pert(4)
-        base(1, 0)
-        base(1, 1)
-        tg(6)
-        cts(3)
-        qg(6)
-        pert(5)
-        base(1, 2)
-        base(1, 3)
-        tg(7)
-        qg(7)
-        pert(6)
-        base(2, 0)
-        base(2, 1)
-        pert(7)
-        base(2, 2)
-        base(2, 3)
-        for m in range(MT):
-            base(3, m)
+        for tk in PLAN:
+            kind = tk[0]
+            if kind == "setup":
+                setup()
+            elif kind == "loadx":
+                load_raw("x%d" % tk[1], input_data[P * tk[1]:P * (tk[1] + 1), :])
+            elif kind == "loadg":
+                load_raw("g%d" % tk[1], prev_grad[P * tk[1]:P * (tk[1] + 1), :])
+            elif kind == "loadwc":
+                loadwc(tk[1])
+            elif kind == "loadsc":
+                loadsc(tk[1], tk[2])
+            elif kind == "lrneg":
+                lrneg()
+            elif kind == "selneg":
+                selneg()
+            elif kind == "lrT":
+                lr_t()
+            elif kind == "sort":
+                sort_words(tk[1], tk[2])
+            elif kind == "tt":
+                transposes(tk[1], tk[2], tk[3])
+            elif kind == "qx":
+                qx(tk[1])
+            elif kind == "qg":
+                qg(tk[1], tk[2])
+            elif kind == "spread":
+                spread(tk[1], tk[2], tk[3])
+            elif kind == "ct":
+                ct(tk[1], tk[2])
+            elif kind == "cpe":
+                cpe(tk[1], tk[2], tk[3])
+            elif kind == "pert":
+                pert(tk[1], tk[2])
+            elif kind == "base":
+                base(tk[1], tk[2])
+            elif kind == "store":
+                store(tk[1], tk[2])
+            else:
+                raise ValueError(kind)

@@ -22,33 +22,32 @@ NCH = OUT // 512
 FLOPS = 2 * 2 * B * IN * OUT
 
 PLAN = (
-    ("setup",), ("sort", "x1", "n"), ("sort", "x0", "n"), ("spread", 2, "s", "s"), ("loadx", 3), ("sort", "x2", "n"),
-    ("loadx", 0), ("lrneg",), ("spread", 0, "v", "v"), ("selneg",), ("loadx", 1), ("lrT",),
-    ("loadx", 2), ("loadg", 1), ("loadsc", 0, 1), ("ct", 2, 2, "v"), ("tt", "x0", "s", "s"), ("qx", 0),
-    ("loadg", 0), ("loadwc", 0), ("loadg", 3), ("tt", "x1", "s", "v"), ("qx", 1), ("loadwc", 1),
-    ("loadg", 2), ("loadsc", 1, 4), ("sort", "g1", "n"), ("sort", "g0", "n"), ("loadg", 5), ("sort", "g6", "n"),
-    ("spread", 1, "s", "s"), ("sort", "x3", "n"), ("loadg", 4), ("loadg", 6), ("ct", 1, 3, "v"), ("ct", 0, 0, "v"),
-    ("tt", "x3", "s", "s"), ("tt", "x2", "s", "s"), ("ct", 1, 0, "v"), ("qx", 3), ("tt", "g1", "s", "s"), ("loadwc", 2),
-    ("qx", 2), ("ct", 0, 1, "v"), ("sort", "g3", "s"), ("ct", 0, 2, "v"), ("spread", 3, "v", "s"), ("cpe", 0, 3, "s"),
-    ("tt", "g0", "s", "v"), ("sort", "g2", "s"), ("ct", 3, 3, "v"), ("base", 0, 0), ("loadwc", 3), ("base", 0, 3),
-    ("ct", 1, 2, "v"), ("base", 0, 1), ("loadg", 9), ("loadg", 10), ("qg", 0, 1), ("cpe", 2, 1, "s"),
-    ("base", 0, 2), ("loadg", 8), ("tt", "g3", "s", "s"), ("ct", 2, 0, "v"), ("tt", "g2", "s", "s"), ("qg", 0, 0),
-    ("sort", "g5", "v"), ("loadg", 7), ("sort", "g4", "s"), ("ct", 1, 1, "v"), ("base", 1, 1), ("base", 1, 2),
-    ("qg", 1, 0), ("base", 1, 3), ("qg", 1, 1), ("loadg", 14), ("pert", 0, 1), ("tt", "g4", "s", "v"),
-    ("tt", "g5", "s", "s"), ("pert", 1, 0), ("ct", 2, 3, "v"), ("base", 2, 0), ("qg", 2, 0), ("ct", 3, 0, "v"),
-    ("pert", 0, 0), ("ct", 3, 2, "v"), ("loadg", 11), ("sort", "g8", "s"), ("sort", "g9", "s"), ("ct", 3, 1, "v"),
-    ("base", 1, 0), ("pert", 1, 1), ("sort", "g10", "s"), ("base", 2, 3), ("qg", 2, 1), ("base", 2, 2),
-    ("loadg", 15), ("base", 2, 1), ("sort", "g7", "s"), ("loadg", 13), ("base", 3, 0), ("loadg", 12),
-    ("tt", "g9", "s", "s"), ("tt", "g6", "v", "s"), ("tt", "g7", "v", "s"), ("qg", 3, 0), ("sort", "g11", "s"), ("sort", "g12", "s"),
-    ("tt", "g8", "v", "v"), ("base", 3, 1), ("qg", 4, 0), ("qg", 3, 1), ("qg", 4, 1), ("base", 3, 2),
-    ("pert", 2, 1), ("tt", "g11", "v", "s"), ("tt", "g10", "s", "s"), ("pert", 2, 0), ("sort", "g13", "s"), ("pert", 3, 0),
-    ("pert", 3, 1), ("qg", 5, 0), ("store", 0, 3), ("tt", "g13", "s", "s"), ("sort", "g15", "s"), ("tt", "g12", "v", "s"),
-    ("store", 1, 1), ("sort", "g14", "s"), ("store", 1, 3), ("store", 0, 2), ("qg", 6, 0), ("qg", 5, 1),
-    ("pert", 4, 1), ("store", 1, 2), ("qg", 6, 1), ("base", 3, 3), ("store", 1, 0), ("pert", 5, 1),
-    ("pert", 5, 0), ("tt", "g15", "s", "v"), ("store", 0, 1), ("tt", "g14", "v", "s"), ("qg", 7, 1), ("qg", 7, 0),
-    ("store", 2, 2), ("pert", 4, 0), ("pert", 6, 0), ("store", 2, 3), ("store", 2, 1), ("pert", 6, 1),
-    ("store", 0, 0), ("pert", 7, 1), ("store", 2, 0), ("pert", 7, 0), ("store", 3, 2), ("store", 3, 3),
-    ("store", 3, 0), ("store", 3, 1),
+    ("setup",), ("loadx", 0), ("tinyload",), ("loadx", 1), ("loadx", 2), ("loadg", 0),
+    ("loadg", 1), ("loadsc", 0, 1), ("loadx", 3), ("loadwc", 0), ("loadg", 3), ("loadg", 2),
+    ("loadsc", 1, 4), ("loadwc", 1), ("loadwc", 2), ("loadg", 4), ("loadg", 8), ("loadg", 5),
+    ("loadg", 9), ("spread", 3, "s", "s"), ("sort", "x0", "v"), ("loadg", 7), ("loadwc", 3), ("lrneg",),
+    ("sort", "x1", "v"), ("loadg", 13), ("spread", 0, "s", "s"), ("spread", 1, "v", "s"), ("tt", "x1", "v", "s"), ("selneg",),
+    ("tt", "x0", "v", "s"), ("lrT",), ("cpe", 2, 3, "s"), ("qx", 1), ("ct", 0, 0, "v"), ("ct", 1, 2, "v"),
+    ("tt", "x2", "s", "s"), ("loadg", 6), ("tt", "g1", "s", "s"), ("ct", 1, 1, "v"), ("qx", 0), ("spread", 2, "s", "s"),
+    ("ct", 0, 1, "v"), ("ct", 0, 2, "v"), ("qx", 2), ("tt", "x3", "s", "s"), ("tt", "g0", "s", "s"), ("loadg", 15),
+    ("loadg", 14), ("loadg", 12), ("ct", 1, 3, "v"), ("qx", 3), ("sort", "g2", "s"), ("ct", 1, 0, "v"),
+    ("qg", 0, 1), ("qg", 0, 0), ("base", 0, 1), ("sort", "g3", "s"), ("loadg", 11), ("loadg", 10),
+    ("ct", 0, 3, "v"), ("ct", 2, 2, "v"), ("ct", 2, 0, "v"), ("base", 0, 2), ("base", 0, 0), ("ct", 3, 3, "v"),
+    ("base", 0, 3), ("tt", "g2", "s", "s"), ("ct", 3, 2, "v"), ("sort", "g4", "s"), ("tt", "g3", "s", "s"), ("base", 1, 2),
+    ("qg", 1, 1), ("pert", 0, 0), ("sort", "g5", "s"), ("qg", 1, 0), ("sort", "g9", "s"), ("base", 2, 2),
+    ("ct", 3, 0, "v"), ("sort", "g7", "v"), ("base", 1, 3), ("base", 2, 3), ("tt", "g4", "s", "s"), ("tt", "g5", "s", "s"),
+    ("ct", 2, 1, "v"), ("base", 1, 0), ("sort", "g6", "s"), ("pert", 0, 1), ("qg", 2, 1), ("tt", "g9", "s", "v"),
+    ("qg", 2, 0), ("tt", "g8", "s", "s"), ("base", 1, 1), ("sort", "g15", "s"), ("qg", 4, 0), ("sort", "g13", "s"),
+    ("sort", "g10", "s"), ("pert", 1, 0), ("store", 0, 0), ("store", 0, 1), ("base", 3, 2), ("pert", 2, 0),
+    ("tt", "g6", "s", "s"), ("qg", 4, 1), ("tt", "g7", "v", "s"), ("qg", 3, 0), ("pert", 1, 1), ("store", 0, 2),
+    ("store", 0, 3), ("ct", 3, 1, "v"), ("sort", "g11", "s"), ("base", 2, 0), ("qg", 3, 1), ("pert", 4, 0),
+    ("sort", "g14", "v"), ("base", 3, 0), ("base", 2, 1), ("sort", "g12", "s"), ("tt", "g10", "s", "s"), ("tt", "g13", "s", "s"),
+    ("pert", 3, 1), ("base", 3, 1), ("tt", "g11", "s", "v"), ("tt", "g12", "s", "v"), ("qg", 5, 1), ("qg", 5, 0),
+    ("tt", "g15", "s", "s"), ("qg", 6, 1), ("qg", 6, 0), ("tt", "g14", "s", "v"), ("qg", 7, 1), ("pert", 4, 1),
+    ("pert", 2, 1), ("store", 1, 2), ("store", 1, 3), ("qg", 7, 0), ("pert", 5, 0), ("store", 2, 0),
+    ("store", 2, 1), ("pert", 6, 0), ("pert", 3, 0), ("store", 1, 0), ("store", 1, 1), ("pert", 6, 1),
+    ("pert", 5, 1), ("store", 2, 2), ("store", 2, 3), ("pert", 7, 0), ("store", 3, 0), ("store", 3, 1),
+    ("pert", 7, 1), ("store", 3, 2), ("base", 3, 3), ("store", 3, 3),
 )
 
 
@@ -102,18 +101,20 @@ def tile_optimizedlinear_kernel(
         def setup():
             make_identity(nc, ident[:])
             nc.vector.memset(b_rows[:].bitcast(I32), 0)
-            nc.scalar.dma_start(out=b_rows[0:1, :], in_=bias.unsqueeze(0))
-            nc.scalar.dma_start(out=b_rows[32:33, :], in_=prev_bias_grad.unsqueeze(0))
             nc.vector.memset(lr_rows[:], 0.0)
-            nc.scalar.dma_start(out=lr_rows[0:MT, :], in_=lr_samples.rearrange("(m p) -> m p", p=P))
             for i in range(2):
                 nc.vector.memset(pick[i][:], 0.0)
                 nc.vector.memset(pick[i][32 * i:32 * i + 1, :], 1.0)
             nc.vector.memset(sel[:], 0.0)
             nc.vector.memset(sel[0:1, :], 1.0)
-            nc.scalar.dma_start(out=sel[32:33, :], in_=lr_samples.unsqueeze(0))
             for a in sorted(planes):
                 nc.vector.memset(planes[a][:].bitcast(I32), 0)
+
+        def tinyload():
+            nc.sync.dma_start(out=b_rows[0:1, :], in_=bias.unsqueeze(0))
+            nc.sync.dma_start(out=b_rows[32:33, :], in_=prev_bias_grad.unsqueeze(0))
+            nc.sync.dma_start(out=lr_rows[0:MT, :], in_=lr_samples.rearrange("(m p) -> m p", p=P))
+            nc.sync.dma_start(out=sel[32:33, :], in_=lr_samples.unsqueeze(0))
 
         def load_raw(key, rows):
             raw[key] = rawp.tile([P, IN], BF16, name="raw")
@@ -250,6 +251,8 @@ def tile_optimizedlinear_kernel(
             kind = tk[0]
             if kind == "setup":
                 setup()
+            elif kind == "tinyload":
+                tinyload()
             elif kind == "loadx":
                 load_raw("x%d" % tk[1], input_data[P * tk[1]:P * (tk[1] + 1), :])
             elif kind == "loadg":

@@ -15,40 +15,16 @@ ADD = mybir.AluOpType.add
 
 P = 128
 B, IN, OUT = 512, 2048, 2048
-G = IN // 512
-MT = B // P
-NPAIR = OUT // 256
-NCH = OUT // 512
+PASSES = IN // 512
+X_TILES = B // P
+G_TILES = OUT // P
+ROW_TILES = X_TILES + G_TILES
+PAIR = 2 * P
+PAIRS = OUT // PAIR
+CHUNK = 512
+CHUNKS = OUT // CHUNK
+RAW_SLOTS = 12
 FLOPS = 2 * 2 * B * IN * OUT
-
-PLAN = (
-    ("setup",), ("loadx", 0), ("tinyload",), ("loadx", 1), ("loadx", 2), ("loadg", 0),
-    ("loadg", 1), ("loadsc", 0, 1), ("loadx", 3), ("loadwc", 0), ("loadg", 3), ("loadg", 2),
-    ("loadsc", 1, 4), ("loadwc", 1), ("loadwc", 2), ("loadg", 4), ("loadg", 8), ("loadg", 5),
-    ("loadg", 9), ("spread", 3, "s", "s"), ("sort", "x0", "v"), ("loadg", 7), ("loadwc", 3), ("lrneg",),
-    ("sort", "x1", "v"), ("loadg", 13), ("spread", 0, "s", "s"), ("spread", 1, "v", "s"), ("tt", "x1", "v", "s"), ("selneg",),
-    ("tt", "x0", "v", "s"), ("lrT",), ("cpe", 2, 3, "s"), ("qx", 1), ("ct", 0, 0, "v"), ("ct", 1, 2, "v"),
-    ("tt", "x2", "s", "s"), ("loadg", 6), ("tt", "g1", "s", "s"), ("ct", 1, 1, "v"), ("qx", 0), ("spread", 2, "s", "s"),
-    ("ct", 0, 1, "v"), ("ct", 0, 2, "v"), ("qx", 2), ("tt", "x3", "s", "s"), ("tt", "g0", "s", "s"), ("loadg", 15),
-    ("loadg", 14), ("loadg", 12), ("ct", 1, 3, "v"), ("qx", 3), ("sort", "g2", "s"), ("ct", 1, 0, "v"),
-    ("qg", 0, 1), ("qg", 0, 0), ("base", 0, 1), ("sort", "g3", "s"), ("loadg", 11), ("loadg", 10),
-    ("ct", 0, 3, "v"), ("ct", 2, 2, "v"), ("ct", 2, 0, "v"), ("base", 0, 2), ("base", 0, 0), ("ct", 3, 3, "v"),
-    ("base", 0, 3), ("tt", "g2", "s", "s"), ("ct", 3, 2, "v"), ("sort", "g4", "s"), ("tt", "g3", "s", "s"), ("base", 1, 2),
-    ("qg", 1, 1), ("pert", 0, 0), ("sort", "g5", "s"), ("qg", 1, 0), ("sort", "g9", "s"), ("base", 2, 2),
-    ("ct", 3, 0, "v"), ("sort", "g7", "v"), ("base", 1, 3), ("base", 2, 3), ("tt", "g4", "s", "s"), ("tt", "g5", "s", "s"),
-    ("ct", 2, 1, "v"), ("base", 1, 0), ("sort", "g6", "s"), ("pert", 0, 1), ("qg", 2, 1), ("tt", "g9", "s", "v"),
-    ("qg", 2, 0), ("tt", "g8", "s", "s"), ("base", 1, 1), ("sort", "g15", "s"), ("qg", 4, 0), ("sort", "g13", "s"),
-    ("sort", "g10", "s"), ("pert", 1, 0), ("store", 0, 0), ("store", 0, 1), ("base", 3, 2), ("pert", 2, 0),
-    ("tt", "g6", "s", "s"), ("qg", 4, 1), ("tt", "g7", "v", "s"), ("qg", 3, 0), ("pert", 1, 1), ("store", 0, 2),
-    ("store", 0, 3), ("ct", 3, 1, "v"), ("sort", "g11", "s"), ("base", 2, 0), ("qg", 3, 1), ("pert", 4, 0),
-    ("sort", "g14", "v"), ("base", 3, 0), ("base", 2, 1), ("sort", "g12", "s"), ("tt", "g10", "s", "s"), ("tt", "g13", "s", "s"),
-    ("pert", 3, 1), ("base", 3, 1), ("tt", "g11", "s", "v"), ("tt", "g12", "s", "v"), ("qg", 5, 1), ("qg", 5, 0),
-    ("tt", "g15", "s", "s"), ("qg", 6, 1), ("qg", 6, 0), ("tt", "g14", "s", "v"), ("qg", 7, 1), ("pert", 4, 1),
-    ("pert", 2, 1), ("store", 1, 2), ("store", 1, 3), ("qg", 7, 0), ("pert", 5, 0), ("store", 2, 0),
-    ("store", 2, 1), ("pert", 6, 0), ("pert", 3, 0), ("store", 1, 0), ("store", 1, 1), ("pert", 6, 1),
-    ("pert", 5, 1), ("store", 2, 2), ("store", 2, 3), ("pert", 7, 0), ("store", 3, 0), ("store", 3, 1),
-    ("pert", 7, 1), ("store", 3, 2), ("base", 3, 3), ("store", 3, 3),
-)
 
 
 def tile_optimizedlinear_kernel(
@@ -57,235 +33,250 @@ def tile_optimizedlinear_kernel(
     nc = tc.nc
     with ExitStack() as ctx:
         keep = ctx.enter_context(tc.tile_pool(name="keep", bufs=1))
-        rawp = ctx.enter_context(tc.tile_pool(name="rawp", bufs=12))
-        sortp = ctx.enter_context(tc.tile_pool(name="sortp", bufs=6))
-        stage = ctx.enter_context(tc.tile_pool(name="stage", bufs=2))
-        pt = ctx.enter_context(tc.psum_pool(name="pt", bufs=4))
-        pa = ctx.enter_context(tc.psum_pool(name="pa", bufs=4))
+        raw_pool = ctx.enter_context(tc.tile_pool(name="raw_pool", bufs=RAW_SLOTS))
+        sorted_pool = ctx.enter_context(tc.tile_pool(name="sorted_pool", bufs=6))
+        grouped_pool = ctx.enter_context(tc.tile_pool(name="grouped_pool", bufs=2))
+        transposed_pool = ctx.enter_context(tc.psum_pool(name="transposed_pool", bufs=4))
+        result_pool = ctx.enter_context(tc.psum_pool(name="result_pool", bufs=4))
         ctx.enter_context(tc.manual_schedule())
 
-        ident = keep.tile([P, P], F32, name="ident")
+        identity = keep.tile([P, P], F32, name="identity")
         lr_rows = keep.tile([P, P], BF16, name="lr_rows")
-        lr_neg = keep.tile([P, P], F32, name="lr_neg")
-        nlr = keep.tile([P, MT], F32, name="nlr")
-        b_rows = keep.tile([P, OUT], BF16, name="b_rows")
-        pick = [keep.tile([P, P], BF16, name="pick%d" % i) for i in range(2)]
-        sel = keep.tile([P, B], BF16, name="sel")
-        w_words = [keep.tile([P, G, 1024], U8, name="w_words%d" % c, align_bytes=64) for c in range(NCH)]
-        xc = [keep.tile([P, G, P], U32, name="xc%d" % m, align_bytes=64) for m in range(MT)]
-        xs = [keep.tile([P, G, P], U8, name="xs%d" % m, align_bytes=64) for m in range(MT)]
-        gc = [keep.tile([P, G, 256], U32, name="gc%d" % h, align_bytes=64) for h in range(NPAIR)]
-        gs = [keep.tile([P, G, 256], U8, name="gs%d" % h, align_bytes=64) for h in range(NPAIR)]
-        bias_bc = keep.tile([P, OUT], BF16, name="bias_bc")
-        pbias_bc = keep.tile([P, OUT], BF16, name="pbias_bc")
-        o = [[keep.tile([P, 512], F32, name="o%d_%d" % (m, c)) for c in range(NCH)] for m in range(MT)]
-        planes = {}
-        plane_of = {}
-        for tk in PLAN:
-            if tk[0] == "loadsc":
-                planes[tk[1]] = keep.tile([P, G, 512 * (tk[2] - tk[1])], U8, name="planes%d" % tk[1], align_bytes=64)
-                for c in range(tk[1], tk[2]):
-                    plane_of[c] = (planes[tk[1]], 512 * (c - tk[1]))
-        scale_rows = weight_scales.rearrange("g q n -> q g n")
+        neg_lr_rows = keep.tile([P, P], F32, name="neg_lr_rows")
+        neg_lr = keep.tile([P, X_TILES], F32, name="neg_lr")
+        bias_rows = keep.tile([P, OUT], BF16, name="bias_rows")
+        pick_row = [keep.tile([P, P], BF16, name="pick_row%d" % i) for i in range(2)]
+        bias_all = [keep.tile([P, OUT], BF16, name="bias_all%d" % i) for i in range(2)]
+        w_words = [keep.tile([P, PASSES, 2 * CHUNK], U8, name="w_words%d" % c, align_bytes=64) for c in range(CHUNKS)]
+        w_scales_first = keep.tile([P, PASSES, CHUNK], U8, name="w_scales_first", align_bytes=64)
+        w_scales_rest = keep.tile([P, PASSES, OUT - CHUNK], U8, name="w_scales_rest", align_bytes=64)
+        x_codes = [keep.tile([P, PASSES, P], U32, name="x_codes%d" % m, align_bytes=64) for m in range(X_TILES)]
+        x_scales = [keep.tile([P, PASSES, P], U8, name="x_scales%d" % m, align_bytes=64) for m in range(X_TILES)]
+        g_codes = [keep.tile([P, PASSES, PAIR], U32, name="g_codes%d" % h, align_bytes=64) for h in range(PAIRS)]
+        g_scales = [keep.tile([P, PASSES, PAIR], U8, name="g_scales%d" % h, align_bytes=64) for h in range(PAIRS)]
+        o = [[keep.tile([P, CHUNK], F32, name="o%d_%d" % (m, c)) for c in range(CHUNKS)] for m in range(X_TILES)]
         raw = {}
-        srt = {}
-        xg = {}
-        gg = {}
+        sorted_words = {}
+        x_grouped = {}
+        g_grouped = {}
+        parts_in = {}
 
-        def evac(engine, dst, src):
-            if engine == "v":
+        def copy(engine, dst, src):
+            if engine == "vector":
                 nc.vector.tensor_copy(out=dst, in_=src)
             else:
                 nc.scalar.copy(out=dst, in_=src)
 
-        def setup():
-            make_identity(nc, ident[:])
-            nc.vector.memset(b_rows[:].bitcast(I32), 0)
-            nc.vector.memset(lr_rows[:], 0.0)
-            for i in range(2):
-                nc.vector.memset(pick[i][:], 0.0)
-                nc.vector.memset(pick[i][32 * i:32 * i + 1, :], 1.0)
-            nc.vector.memset(sel[:], 0.0)
-            nc.vector.memset(sel[0:1, :], 1.0)
-            for a in sorted(planes):
-                nc.vector.memset(planes[a][:].bitcast(I32), 0)
+        def load_rows(a):
+            if a < X_TILES:
+                rows = input_data[P * a:P * (a + 1), :]
+            else:
+                rows = prev_grad[P * (a - X_TILES):P * (a - X_TILES + 1), :]
+            raw[a] = raw_pool.tile([P, IN], BF16, name="raw")
+            nc.sync.dma_start(out=raw[a][:], in_=rows)
 
-        def tinyload():
-            nc.sync.dma_start(out=b_rows[0:1, :], in_=bias.unsqueeze(0))
-            nc.sync.dma_start(out=b_rows[32:33, :], in_=prev_bias_grad.unsqueeze(0))
-            nc.sync.dma_start(out=lr_rows[0:MT, :], in_=lr_samples.rearrange("(m p) -> m p", p=P))
-            nc.sync.dma_start(out=sel[32:33, :], in_=lr_samples.unsqueeze(0))
+        def slot_free(a):
+            if a + RAW_SLOTS < ROW_TILES:
+                load_rows(a + RAW_SLOTS)
 
-        def load_raw(key, rows):
-            raw[key] = rawp.tile([P, IN], BF16, name="raw")
-            nc.sync.dma_start(out=raw[key][:], in_=rows)
+        def load_small_vectors():
+            nc.sync.dma_start(out=bias_rows[0:1, :], in_=bias.unsqueeze(0))
+            nc.sync.dma_start(out=bias_rows[32:33, :], in_=prev_bias_grad.unsqueeze(0))
+            nc.sync.dma_start(out=lr_rows[0:X_TILES, :], in_=lr_samples.rearrange("(m p) -> m p", p=P))
 
-        def loadwc(c):
+        def load_weight(c):
             nc.sync.dma_start(
                 out=w_words[c][:].bitcast(I32),
-                in_=weight_words[:, :, 1024 * c:1024 * (c + 1)].rearrange("g p b -> p g b").bitcast(I32),
+                in_=weight_words[:, :, 2 * CHUNK * c:2 * CHUNK * (c + 1)].rearrange("g p b -> p g b").bitcast(I32),
             )
 
-        def loadsc(a, b):
+        def load_weight_scales(tile, first_column, last_column):
+            rows = weight_scales.rearrange("g q n -> q g n")
             for r in range(4):
                 nc.sync.dma_start(
-                    out=planes[a][r:P:32, :, :].bitcast(I32),
-                    in_=scale_rows[r:16:4, :, 512 * a:512 * b].bitcast(I32),
+                    out=tile[r:P:32, :, :].bitcast(I32), in_=rows[r:16:4, :, first_column:last_column].bitcast(I32)
                 )
 
-        def lrneg():
-            nc.vector.tensor_scalar(out=lr_neg[:], in0=lr_rows[:], scalar1=-1.0, scalar2=None, op0=MULT)
+        def part_done(m, c):
+            parts_in[(m, c)] = parts_in.get((m, c), 0) + 1
+            if parts_in[(m, c)] == 3:
+                nc.sync.dma_start(out=out[P * m:P * (m + 1), CHUNK * c:CHUNK * (c + 1)], in_=o[m][c][:])
 
-        def selneg():
-            nc.vector.tensor_scalar(out=sel[32:33, :], in0=sel[32:33, :], scalar1=-1.0, scalar2=None, op0=MULT)
+        def strided_words(a):
+            return raw[a][:].bitcast(F32).rearrange("r (g p u) -> r g u p", g=PASSES, u=2)
 
-        def lr_t():
-            lr_bank = pt.tile([P, 2, 2, P], F32, name="tbank")
-            nc.tensor.transpose(lr_bank[:, 0, 0, :], lr_neg[:], ident[:])
-            nc.vector.tensor_copy(out=nlr[:], in_=lr_bank[:, 0, 0, 0:MT])
+        def sort_words(a, engine):
+            sorted_words[a] = sorted_pool.tile([P, PASSES, 2, P], F32, name="sorted_words")
+            copy(engine, sorted_words[a][:], strided_words(a))
+            slot_free(a)
 
-        def word_view(key):
-            return raw[key][:].bitcast(F32).rearrange("r (g p u) -> r g u p", g=G, u=2)
+        def sort_pair(h):
+            for j in (2 * h, 2 * h + 1):
+                sort_words(X_TILES + j, "vector" if j % 3 == 2 else "scalar")
 
-        def sort_words(key, engine):
-            if engine != "n":
-                sorted_words = sortp.tile([P, G, 2, P], F32, name="srt")
-                evac(engine, sorted_words[:], word_view(key))
-                srt[key] = sorted_words
-
-        def transposes(key, e0, e1):
-            idx = int(key[1:])
-            if key[0] == "x":
-                xg[idx] = stage.tile([P, G, P, 4], BF16, name="xg", align_bytes=64)
-                dst_words = xg[idx][:].bitcast(F32)
-                rows = slice(0, P)
-            else:
-                h = idx // 2
-                if h not in gg:
-                    gg[h] = stage.tile([P, G, 256, 4], BF16, name="gg", align_bytes=64)
-                dst_words = gg[h][:].bitcast(F32)
-                rows = slice(P * (idx % 2), P * (idx % 2 + 1))
-            words = srt[key] if key in srt else word_view(key)
-            for gp in range(2):
-                tbank = pt.tile([P, 2, 2, P], F32, name="tbank")
-                for g2 in range(2):
+        def transpose_tile(a, grouped_words, rows):
+            words = sorted_words[a] if a in sorted_words else strided_words(a)
+            for half in range(2):
+                bank = transposed_pool.tile([P, 2, 2, P], F32, name="transposed")
+                for g in range(2):
                     for u in range(2):
-                        nc.tensor.transpose(tbank[:, g2, u, :], words[:, 2 * gp + g2, u, :], ident[:])
-                evac((e0, e1)[gp], dst_words[:, 2 * gp:2 * gp + 2, rows, :], tbank[:].rearrange("p g u r -> p g r u"))
+                        nc.tensor.transpose(bank[:, g, u, :], words[:, 2 * half + g, u, :], identity[:])
+                copy("scalar", grouped_words[:, 2 * half:2 * half + 2, rows, :], bank[:].rearrange("p g u r -> p g r u"))
+            if a not in sorted_words:
+                slot_free(a)
 
-        def qx(m):
+        def transpose_x(m):
+            x_grouped[m] = grouped_pool.tile([P, PASSES, P, 4], BF16, name="x_grouped", align_bytes=64)
+            transpose_tile(m, x_grouped[m][:].bitcast(F32), slice(0, P))
+
+        def quantise_x(m):
             nc.vector.quantize_mx(
-                out=xc[m][:].rearrange("p g r -> p (g r)").bitcast(FP8X4),
-                scales=xs[m][:].rearrange("p g r -> p (g r)"),
-                in_=xg[m][:].rearrange("p g r t -> p (g r t)"),
+                out=x_codes[m][:].rearrange("p g r -> p (g r)").bitcast(FP8X4),
+                scales=x_scales[m][:].rearrange("p g r -> p (g r)"),
+                in_=x_grouped[m][:].rearrange("p g r t -> p (g r t)"),
             )
 
-        def qg(h, a):
-            nc.vector.quantize_mx(
-                out=gc[h][:, 2 * a:2 * a + 2, :].rearrange("p g r -> p (g r)").bitcast(FP8X4),
-                scales=gs[h][:, 2 * a:2 * a + 2, :].rearrange("p g r -> p (g r)"),
-                in_=gg[h][:, 2 * a:2 * a + 2, :, :].rearrange("p g r t -> p (g r t)"),
-            )
-
-        def spread(c, e0, e1):
-            cols = slice(512 * c, 512 * (c + 1))
+        def transpose_pair(h):
+            g_grouped[h] = grouped_pool.tile([P, PASSES, PAIR, 4], BF16, name="g_grouped", align_bytes=64)
             for i in range(2):
-                bank = pa.tile([P, 512], F32, name="acc")
-                nc.tensor.matmul(out=bank[:], lhsT=pick[i][:], rhs=b_rows[:, cols], start=True, stop=True)
-                evac((e0, e1)[i], (bias_bc, pbias_bc)[i][:, cols], bank[:])
+                transpose_tile(X_TILES + 2 * h + i, g_grouped[h][:].bitcast(F32), slice(P * i, P * (i + 1)))
 
-        def ct(c, m):
-            cols = slice(512 * c, 512 * (c + 1))
-            nc.vector.scalar_tensor_tensor(
-                out=o[m][c][:], in0=pbias_bc[:, cols], scalar=nlr[:, m:m + 1], in1=bias_bc[:, cols], op0=MULT, op1=ADD
-            )
-
-        def cpe(c, m, engine):
-            bank = pa.tile([P, 512], F32, name="acc")
-            nc.tensor.matmul(
-                out=bank[:], lhsT=sel[:, P * m:P * (m + 1)], rhs=b_rows[:, 512 * c:512 * (c + 1)], start=True, stop=True
-            )
-            evac(engine, o[m][c][:], bank[:])
-
-        def pert(h, mp):
-            c, half = h // 2, h % 2
-            bank = pa.tile([P, 512], F32, name="acc")
-            for i in range(2):
-                m = 2 * mp + i
-                for g in range(G):
-                    nc.tensor.matmul_mx(
-                        out=bank[:, 256 * i:256 * (i + 1)],
-                        lhsT=xc[m][:, g, :].bitcast(FP8X4),
-                        lhsT_scale=xs[m][:, g, :],
-                        rhs=gc[h][:, g, :].bitcast(FP8X4),
-                        rhs_scale=gs[h][:, g, :],
-                        start=(g == 0),
-                        stop=(g == G - 1),
-                    )
-            for i in range(2):
-                m = 2 * mp + i
-                dst = o[m][c][:, 256 * half:256 * (half + 1)]
-                nc.vector.scalar_tensor_tensor(
-                    out=dst, in0=bank[:, 256 * i:256 * (i + 1)], scalar=nlr[:, m:m + 1], in1=dst, op0=MULT, op1=ADD
+        def quantise_pair(h):
+            for half in range(2):
+                passes = slice(2 * half, 2 * half + 2)
+                nc.vector.quantize_mx(
+                    out=g_codes[h][:, passes, :].rearrange("p g r -> p (g r)").bitcast(FP8X4),
+                    scales=g_scales[h][:, passes, :].rearrange("p g r -> p (g r)"),
+                    in_=g_grouped[h][:, passes, :, :].rearrange("p g r t -> p (g r t)"),
                 )
+
+        def spread_biases(c, engines):
+            columns = slice(CHUNK * c, CHUNK * (c + 1))
+            for i in range(2):
+                bank = result_pool.tile([P, CHUNK], F32, name="result")
+                nc.tensor.matmul(out=bank[:], lhsT=pick_row[i][:], rhs=bias_rows[:, columns], start=True, stop=True)
+                copy(engines[i], bias_all[i][:, columns], bank[:])
+
+        def bias_term(c, m):
+            columns = slice(CHUNK * c, CHUNK * (c + 1))
+            nc.vector.scalar_tensor_tensor(
+                out=o[m][c][:], in0=bias_all[1][:, columns], scalar=neg_lr[:, m:m + 1], in1=bias_all[0][:, columns],
+                op0=MULT, op1=ADD,
+            )
+
+        def perturbation(h):
+            c, half = h // 2, h % 2
+            for first in range(0, X_TILES, 2):
+                bank = result_pool.tile([P, CHUNK], F32, name="result")
+                for i in range(2):
+                    m = first + i
+                    for g in range(PASSES):
+                        nc.tensor.matmul_mx(
+                            out=bank[:, PAIR * i:PAIR * (i + 1)],
+                            lhsT=x_codes[m][:, g, :].bitcast(FP8X4),
+                            lhsT_scale=x_scales[m][:, g, :],
+                            rhs=g_codes[h][:, g, :].bitcast(FP8X4),
+                            rhs_scale=g_scales[h][:, g, :],
+                            start=(g == 0),
+                            stop=(g == PASSES - 1),
+                        )
+                for i in range(2):
+                    m = first + i
+                    dst = o[m][c][:, PAIR * half:PAIR * (half + 1)]
+                    nc.vector.scalar_tensor_tensor(
+                        out=dst, in0=bank[:, PAIR * i:PAIR * (i + 1)], scalar=neg_lr[:, m:m + 1], in1=dst,
+                        op0=MULT, op1=ADD,
+                    )
+                    part_done(m, c)
 
         def base(c, m):
-            bank = pa.tile([P, 512], F32, name="acc")
-            plane, off = plane_of[c]
-            for g in range(G):
+            bank = result_pool.tile([P, CHUNK], F32, name="result")
+            for g in range(PASSES):
+                if c == 0:
+                    scales = w_scales_first[:, g, :]
+                else:
+                    scales = w_scales_rest[:, g, CHUNK * (c - 1):CHUNK * c]
                 nc.tensor.matmul_mx(
                     out=bank[:],
-                    lhsT=xc[m][:, g, :].bitcast(FP8X4),
-                    lhsT_scale=xs[m][:, g, :],
+                    lhsT=x_codes[m][:, g, :].bitcast(FP8X4),
+                    lhsT_scale=x_scales[m][:, g, :],
                     rhs=w_words[c][:, g, :].bitcast(FP4X4),
-                    rhs_scale=plane[:, g, off:off + 512],
+                    rhs_scale=scales,
                     start=(g == 0),
-                    stop=(g == G - 1),
+                    stop=(g == PASSES - 1),
                 )
             nc.vector.tensor_tensor(out=o[m][c][:], in0=bank[:], in1=o[m][c][:], op=ADD)
+            part_done(m, c)
 
-        def store(c, m):
-            nc.sync.dma_start(out=out[P * m:P * (m + 1), 512 * c:512 * (c + 1)], in_=o[m][c][:])
+        make_identity(nc, identity[:])
+        nc.vector.memset(bias_rows[:].bitcast(I32), 0)
+        nc.vector.memset(lr_rows[:], 0.0)
+        for i in range(2):
+            nc.vector.memset(pick_row[i][:], 0.0)
+            nc.vector.memset(pick_row[i][32 * i:32 * i + 1, :], 1.0)
+        nc.vector.memset(w_scales_first[:].bitcast(I32), 0)
+        nc.vector.memset(w_scales_rest[:].bitcast(I32), 0)
 
-        for tk in PLAN:
-            kind = tk[0]
-            if kind == "setup":
-                setup()
-            elif kind == "tinyload":
-                tinyload()
-            elif kind == "loadx":
-                load_raw("x%d" % tk[1], input_data[P * tk[1]:P * (tk[1] + 1), :])
-            elif kind == "loadg":
-                load_raw("g%d" % tk[1], prev_grad[P * tk[1]:P * (tk[1] + 1), :])
-            elif kind == "loadwc":
-                loadwc(tk[1])
-            elif kind == "loadsc":
-                loadsc(tk[1], tk[2])
-            elif kind == "lrneg":
-                lrneg()
-            elif kind == "selneg":
-                selneg()
-            elif kind == "lrT":
-                lr_t()
-            elif kind == "sort":
-                sort_words(tk[1], tk[2])
-            elif kind == "tt":
-                transposes(tk[1], tk[2], tk[3])
-            elif kind == "qx":
-                qx(tk[1])
-            elif kind == "qg":
-                qg(tk[1], tk[2])
-            elif kind == "spread":
-                spread(tk[1], tk[2], tk[3])
-            elif kind == "ct":
-                ct(tk[1], tk[2])
-            elif kind == "cpe":
-                cpe(tk[1], tk[2], tk[3])
-            elif kind == "pert":
-                pert(tk[1], tk[2])
-            elif kind == "base":
-                base(tk[1], tk[2])
-            elif kind == "store":
-                store(tk[1], tk[2])
-            else:
-                raise ValueError(kind)
+        load_rows(0)
+        load_small_vectors()
+        load_rows(1)
+        load_rows(2)
+        load_weight_scales(w_scales_first, 0, CHUNK)
+        load_rows(3)
+        load_weight(0)
+        load_weight(1)
+        load_rows(4)
+        load_rows(5)
+        load_rows(6)
+        load_weight_scales(w_scales_rest, CHUNK, OUT)
+        load_rows(7)
+        load_weight(2)
+        load_rows(8)
+        load_rows(9)
+        load_weight(3)
+        load_rows(10)
+        load_rows(11)
+
+        nc.vector.tensor_scalar(out=neg_lr_rows[:], in0=lr_rows[:], scalar1=-1.0, scalar2=None, op0=MULT)
+        transpose_x(0)
+        sort_words(1, "vector")
+        spread_biases(0, ("scalar", "scalar"))
+        quantise_x(0)
+        spread_biases(1, ("scalar", "vector"))
+        lr_bank = transposed_pool.tile([P, 2, 2, P], F32, name="transposed")
+        nc.tensor.transpose(lr_bank[:, 0, 0, :], neg_lr_rows[:], identity[:])
+        nc.vector.tensor_copy(out=neg_lr[:], in_=lr_bank[:, 0, 0, 0:X_TILES])
+        transpose_x(1)
+        quantise_x(1)
+        bias_term(0, 0)
+        transpose_x(2)
+        transpose_x(3)
+        quantise_x(2)
+        bias_term(0, 1)
+        bias_term(0, 2)
+        quantise_x(3)
+        spread_biases(2, ("scalar", "scalar"))
+        bias_term(0, 3)
+        sort_pair(0)
+        for m in range(X_TILES):
+            base(0, m)
+        spread_biases(3, ("vector", "scalar"))
+
+        later_bases = [(c, m) for c in range(1, CHUNKS) for m in range(X_TILES)]
+        bases_in_round = [2, 1, 1, 1, 1, 1, 1, 2]
+        for h in range(PAIRS):
+            transpose_pair(h)
+            if h + 1 < PAIRS:
+                sort_pair(h + 1)
+            if h % 2 == 0 and h // 2 + 1 < CHUNKS:
+                for m in range(X_TILES):
+                    bias_term(h // 2 + 1, m)
+            quantise_pair(h)
+            if h > 0:
+                perturbation(h - 1)
+            first = sum(bases_in_round[:h])
+            for c, m in later_bases[first:first + bases_in_round[h]]:
+                base(c, m)
+        perturbation(PAIRS - 1)
+        for c, m in later_bases[sum(bases_in_round):]:
+            base(c, m)

@@ -19,11 +19,11 @@ PASSES = IN // 512
 X_TILES = B // P
 G_TILES = OUT // P
 ROW_TILES = X_TILES + G_TILES
-PAIR = 2 * P
-PAIRS = OUT // PAIR
 CHUNK = 512
 CHUNKS = OUT // CHUNK
-RAW_SLOTS = 12
+QUAD = CHUNK // P
+RAW_SLOTS = 10
+SORTED_SLOTS = 2 * QUAD
 FLOPS = 2 * 2 * B * IN * OUT
 
 
@@ -34,10 +34,9 @@ def tile_optimizedlinear_kernel(
     with ExitStack() as ctx:
         keep = ctx.enter_context(tc.tile_pool(name="keep", bufs=1))
         raw_pool = ctx.enter_context(tc.tile_pool(name="raw_pool", bufs=RAW_SLOTS))
-        sorted_pool = ctx.enter_context(tc.tile_pool(name="sorted_pool", bufs=6))
+        sorted_pool = ctx.enter_context(tc.tile_pool(name="sorted_pool", bufs=SORTED_SLOTS))
         grouped_pool = ctx.enter_context(tc.tile_pool(name="grouped_pool", bufs=2))
-        transposed_pool = ctx.enter_context(tc.psum_pool(name="transposed_pool", bufs=4))
-        result_pool = ctx.enter_context(tc.psum_pool(name="result_pool", bufs=4))
+        banks = ctx.enter_context(tc.psum_pool(name="banks", bufs=8))
         ctx.enter_context(tc.manual_schedule())
 
         identity = keep.tile([P, P], F32, name="identity")
@@ -45,21 +44,20 @@ def tile_optimizedlinear_kernel(
         neg_lr_rows = keep.tile([P, P], F32, name="neg_lr_rows")
         neg_lr = keep.tile([P, X_TILES], F32, name="neg_lr")
         bias_rows = keep.tile([P, OUT], BF16, name="bias_rows")
-        pick_row = [keep.tile([P, P], BF16, name="pick_row%d" % i) for i in range(2)]
-        bias_all = [keep.tile([P, OUT], BF16, name="bias_all%d" % i) for i in range(2)]
+        first_row = keep.tile([P, P], BF16, name="first_row")
+        bias_all = keep.tile([P, OUT], BF16, name="bias_all")
+        prev_bias_all = keep.tile([P, OUT], BF16, name="prev_bias_all")
         w_words = [keep.tile([P, PASSES, 2 * CHUNK], U8, name="w_words%d" % c, align_bytes=64) for c in range(CHUNKS)]
-        w_scales_first = keep.tile([P, PASSES, CHUNK], U8, name="w_scales_first", align_bytes=64)
-        w_scales_rest = keep.tile([P, PASSES, OUT - CHUNK], U8, name="w_scales_rest", align_bytes=64)
+        w_scales = [keep.tile([P, PASSES, CHUNK], U8, name="w_scales%d" % c, align_bytes=64) for c in range(CHUNKS)]
         x_codes = [keep.tile([P, PASSES, P], U32, name="x_codes%d" % m, align_bytes=64) for m in range(X_TILES)]
         x_scales = [keep.tile([P, PASSES, P], U8, name="x_scales%d" % m, align_bytes=64) for m in range(X_TILES)]
-        g_codes = [keep.tile([P, PASSES, PAIR], U32, name="g_codes%d" % h, align_bytes=64) for h in range(PAIRS)]
-        g_scales = [keep.tile([P, PASSES, PAIR], U8, name="g_scales%d" % h, align_bytes=64) for h in range(PAIRS)]
+        g_codes = [keep.tile([P, PASSES, CHUNK], U32, name="g_codes%d" % c, align_bytes=64) for c in range(CHUNKS)]
+        g_scales = [keep.tile([P, PASSES, CHUNK], U8, name="g_scales%d" % c, align_bytes=64) for c in range(CHUNKS)]
+        g_grouped = keep.tile([P, PASSES, CHUNK, 4], BF16, name="g_grouped", align_bytes=64)
         o = [[keep.tile([P, CHUNK], F32, name="o%d_%d" % (m, c)) for c in range(CHUNKS)] for m in range(X_TILES)]
         raw = {}
         sorted_words = {}
         x_grouped = {}
-        g_grouped = {}
-        parts_in = {}
 
         def copy(engine, dst, src):
             if engine == "vector":
@@ -79,28 +77,17 @@ def tile_optimizedlinear_kernel(
             if a + RAW_SLOTS < ROW_TILES:
                 load_rows(a + RAW_SLOTS)
 
-        def load_small_vectors():
-            nc.sync.dma_start(out=bias_rows[0:1, :], in_=bias.unsqueeze(0))
-            nc.sync.dma_start(out=bias_rows[32:33, :], in_=prev_bias_grad.unsqueeze(0))
-            nc.sync.dma_start(out=lr_rows[0:X_TILES, :], in_=lr_samples.rearrange("(m p) -> m p", p=P))
-
         def load_weight(c):
+            rows = weight_scales.rearrange("g q n -> q g n")
+            for r in range(4):
+                nc.sync.dma_start(
+                    out=w_scales[c][r:P:32, :, :].bitcast(I32),
+                    in_=rows[r:16:4, :, CHUNK * c:CHUNK * (c + 1)].bitcast(I32),
+                )
             nc.sync.dma_start(
                 out=w_words[c][:].bitcast(I32),
                 in_=weight_words[:, :, 2 * CHUNK * c:2 * CHUNK * (c + 1)].rearrange("g p b -> p g b").bitcast(I32),
             )
-
-        def load_weight_scales(tile, first_column, last_column):
-            rows = weight_scales.rearrange("g q n -> q g n")
-            for r in range(4):
-                nc.sync.dma_start(
-                    out=tile[r:P:32, :, :].bitcast(I32), in_=rows[r:16:4, :, first_column:last_column].bitcast(I32)
-                )
-
-        def part_done(m, c):
-            parts_in[(m, c)] = parts_in.get((m, c), 0) + 1
-            if parts_in[(m, c)] == 3:
-                nc.sync.dma_start(out=out[P * m:P * (m + 1), CHUNK * c:CHUNK * (c + 1)], in_=o[m][c][:])
 
         def strided_words(a):
             return raw[a][:].bitcast(F32).rearrange("r (g p u) -> r g u p", g=PASSES, u=2)
@@ -110,24 +97,19 @@ def tile_optimizedlinear_kernel(
             copy(engine, sorted_words[a][:], strided_words(a))
             slot_free(a)
 
-        def sort_pair(h):
-            for j in (2 * h, 2 * h + 1):
-                sort_words(X_TILES + j, "vector" if j % 3 == 2 else "scalar")
-
-        def transpose_tile(a, grouped_words, rows):
+        def transpose_half(a, half, grouped_words, rows, engine):
             words = sorted_words[a] if a in sorted_words else strided_words(a)
-            for half in range(2):
-                bank = transposed_pool.tile([P, 2, 2, P], F32, name="transposed")
-                for g in range(2):
-                    for u in range(2):
-                        nc.tensor.transpose(bank[:, g, u, :], words[:, 2 * half + g, u, :], identity[:])
-                copy("scalar", grouped_words[:, 2 * half:2 * half + 2, rows, :], bank[:].rearrange("p g u r -> p g r u"))
-            if a not in sorted_words:
-                slot_free(a)
+            bank = banks.tile([P, 2, 2, P], F32, name="bank")
+            for g in range(2):
+                for u in range(2):
+                    nc.tensor.transpose(bank[:, g, u, :], words[:, 2 * half + g, u, :], identity[:])
+            copy(engine, grouped_words[:, 2 * half:2 * half + 2, rows, :], bank[:].rearrange("p g u r -> p g r u"))
 
         def transpose_x(m):
             x_grouped[m] = grouped_pool.tile([P, PASSES, P, 4], BF16, name="x_grouped", align_bytes=64)
-            transpose_tile(m, x_grouped[m][:].bitcast(F32), slice(0, P))
+            transpose_half(m, 0, x_grouped[m][:].bitcast(F32), slice(0, P), "scalar")
+            transpose_half(m, 1, x_grouped[m][:].bitcast(F32), slice(0, P), "vector")
+            slot_free(m)
 
         def quantise_x(m):
             nc.vector.quantize_mx(
@@ -136,147 +118,122 @@ def tile_optimizedlinear_kernel(
                 in_=x_grouped[m][:].rearrange("p g r t -> p (g r t)"),
             )
 
-        def transpose_pair(h):
-            g_grouped[h] = grouped_pool.tile([P, PASSES, PAIR, 4], BF16, name="g_grouped", align_bytes=64)
-            for i in range(2):
-                transpose_tile(X_TILES + 2 * h + i, g_grouped[h][:].bitcast(F32), slice(P * i, P * (i + 1)))
+        def transpose_quad(c):
+            words = g_grouped[:].bitcast(F32)
+            if c == 0:
+                order = [(i, half) for i in range(QUAD) for half in range(2)]
+            else:
+                order = [(i, half) for half in range(2) for i in range(QUAD)]
+            for i, half in order:
+                engine = "vector" if c == 0 and half == 1 else "scalar"
+                transpose_half(X_TILES + QUAD * c + i, half, words, slice(P * i, P * (i + 1)), engine)
 
-        def quantise_pair(h):
-            for half in range(2):
-                passes = slice(2 * half, 2 * half + 2)
-                nc.vector.quantize_mx(
-                    out=g_codes[h][:, passes, :].rearrange("p g r -> p (g r)").bitcast(FP8X4),
-                    scales=g_scales[h][:, passes, :].rearrange("p g r -> p (g r)"),
-                    in_=g_grouped[h][:, passes, :, :].rearrange("p g r t -> p (g r t)"),
-                )
-
-        def spread_biases(c, engines):
-            columns = slice(CHUNK * c, CHUNK * (c + 1))
-            for i in range(2):
-                bank = result_pool.tile([P, CHUNK], F32, name="result")
-                nc.tensor.matmul(out=bank[:], lhsT=pick_row[i][:], rhs=bias_rows[:, columns], start=True, stop=True)
-                copy(engines[i], bias_all[i][:, columns], bank[:])
-
-        def bias_term(c, m):
-            columns = slice(CHUNK * c, CHUNK * (c + 1))
-            nc.vector.scalar_tensor_tensor(
-                out=o[m][c][:], in0=bias_all[1][:, columns], scalar=neg_lr[:, m:m + 1], in1=bias_all[0][:, columns],
-                op0=MULT, op1=ADD,
+        def quantise_quad(c, half):
+            passes = slice(2 * half, 2 * half + 2)
+            nc.vector.quantize_mx(
+                out=g_codes[c][:, passes, :].rearrange("p g r -> p (g r)").bitcast(FP8X4),
+                scales=g_scales[c][:, passes, :].rearrange("p g r -> p (g r)"),
+                in_=g_grouped[:, passes, :, :].rearrange("p g r t -> p (g r t)"),
             )
 
-        def perturbation(h):
-            c, half = h // 2, h % 2
-            for first in range(0, X_TILES, 2):
-                bank = result_pool.tile([P, CHUNK], F32, name="result")
-                for i in range(2):
-                    m = first + i
-                    for g in range(PASSES):
-                        nc.tensor.matmul_mx(
-                            out=bank[:, PAIR * i:PAIR * (i + 1)],
-                            lhsT=x_codes[m][:, g, :].bitcast(FP8X4),
-                            lhsT_scale=x_scales[m][:, g, :],
-                            rhs=g_codes[h][:, g, :].bitcast(FP8X4),
-                            rhs_scale=g_scales[h][:, g, :],
-                            start=(g == 0),
-                            stop=(g == PASSES - 1),
-                        )
-                for i in range(2):
-                    m = first + i
-                    dst = o[m][c][:, PAIR * half:PAIR * (half + 1)]
-                    nc.vector.scalar_tensor_tensor(
-                        out=dst, in0=bank[:, PAIR * i:PAIR * (i + 1)], scalar=neg_lr[:, m:m + 1], in1=dst,
-                        op0=MULT, op1=ADD,
-                    )
-                    part_done(m, c)
+        def spread_bias(c, engine):
+            columns = slice(CHUNK * c, CHUNK * (c + 1))
+            bank = banks.tile([P, CHUNK], F32, name="bank")
+            nc.tensor.matmul(out=bank[:], lhsT=first_row[:], rhs=bias_rows[:, columns], start=True, stop=True)
+            copy(engine, bias_all[:, columns], bank[:])
 
-        def base(c, m):
-            bank = result_pool.tile([P, CHUNK], F32, name="result")
+        def product(m, rhs, rhs_scale):
+            bank = banks.tile([P, CHUNK], F32, name="bank")
             for g in range(PASSES):
-                if c == 0:
-                    scales = w_scales_first[:, g, :]
-                else:
-                    scales = w_scales_rest[:, g, CHUNK * (c - 1):CHUNK * c]
                 nc.tensor.matmul_mx(
                     out=bank[:],
                     lhsT=x_codes[m][:, g, :].bitcast(FP8X4),
                     lhsT_scale=x_scales[m][:, g, :],
-                    rhs=w_words[c][:, g, :].bitcast(FP4X4),
-                    rhs_scale=scales,
+                    rhs=rhs[g],
+                    rhs_scale=rhs_scale[g],
                     start=(g == 0),
                     stop=(g == PASSES - 1),
                 )
-            nc.vector.tensor_tensor(out=o[m][c][:], in0=bank[:], in1=o[m][c][:], op=ADD)
-            part_done(m, c)
+            return bank
+
+        def base(c, m):
+            bank = product(
+                m, [w_words[c][:, g, :].bitcast(FP4X4) for g in range(PASSES)], [w_scales[c][:, g, :] for g in range(PASSES)]
+            )
+            nc.vector.tensor_tensor(out=o[m][c][:], in0=bank[:], in1=bias_all[:, CHUNK * c:CHUNK * (c + 1)], op=ADD)
+
+        def prev_bias_term(c, m):
+            nc.vector.scalar_tensor_tensor(
+                out=o[m][c][:], in0=prev_bias_all[:, CHUNK * c:CHUNK * (c + 1)], scalar=neg_lr[:, m:m + 1], in1=o[m][c][:],
+                op0=MULT, op1=ADD,
+            )
+
+        def perturbation(c, m):
+            bank = product(
+                m, [g_codes[c][:, g, :].bitcast(FP8X4) for g in range(PASSES)], [g_scales[c][:, g, :] for g in range(PASSES)]
+            )
+            nc.vector.scalar_tensor_tensor(
+                out=o[m][c][:], in0=bank[:], scalar=neg_lr[:, m:m + 1], in1=o[m][c][:], op0=MULT, op1=ADD,
+            )
+            nc.sync.dma_start(out=out[P * m:P * (m + 1), CHUNK * c:CHUNK * (c + 1)], in_=o[m][c][:])
 
         make_identity(nc, identity[:])
         nc.vector.memset(bias_rows[:].bitcast(I32), 0)
         nc.vector.memset(lr_rows[:], 0.0)
-        for i in range(2):
-            nc.vector.memset(pick_row[i][:], 0.0)
-            nc.vector.memset(pick_row[i][32 * i:32 * i + 1, :], 1.0)
-        nc.vector.memset(w_scales_first[:].bitcast(I32), 0)
-        nc.vector.memset(w_scales_rest[:].bitcast(I32), 0)
+        nc.vector.memset(first_row[:], 0.0)
+        nc.vector.memset(first_row[0:1, :], 1.0)
+        for c in range(CHUNKS):
+            nc.vector.memset(w_scales[c][:].bitcast(I32), 0)
 
-        load_rows(0)
-        load_small_vectors()
-        load_rows(1)
-        load_rows(2)
-        load_weight_scales(w_scales_first, 0, CHUNK)
-        load_rows(3)
+        nc.sync.dma_start(out=bias_rows[0:1, :], in_=bias.unsqueeze(0))
+        nc.sync.dma_start(out=lr_rows[0:X_TILES, :], in_=lr_samples.rearrange("(m p) -> m p", p=P))
+        for m in range(X_TILES):
+            load_rows(m)
         load_weight(0)
+        for i in range(QUAD):
+            load_rows(X_TILES + i)
         load_weight(1)
-        load_rows(4)
-        load_rows(5)
-        load_rows(6)
-        load_weight_scales(w_scales_rest, CHUNK, OUT)
-        load_rows(7)
+        nc.sync.dma_start(out=prev_bias_all[:], in_=prev_bias_grad.partition_broadcast(P))
+        load_rows(X_TILES + QUAD)
+        load_rows(X_TILES + QUAD + 1)
         load_weight(2)
-        load_rows(8)
-        load_rows(9)
-        load_weight(3)
-        load_rows(10)
-        load_rows(11)
 
         nc.vector.tensor_scalar(out=neg_lr_rows[:], in0=lr_rows[:], scalar1=-1.0, scalar2=None, op0=MULT)
-        transpose_x(0)
-        sort_words(1, "vector")
-        spread_biases(0, ("scalar", "scalar"))
-        quantise_x(0)
-        spread_biases(1, ("scalar", "vector"))
-        lr_bank = transposed_pool.tile([P, 2, 2, P], F32, name="transposed")
+        spread_bias(0, "scalar")
+        lr_bank = banks.tile([P, 2, 2, P], F32, name="bank")
         nc.tensor.transpose(lr_bank[:, 0, 0, :], neg_lr_rows[:], identity[:])
         nc.vector.tensor_copy(out=neg_lr[:], in_=lr_bank[:, 0, 0, 0:X_TILES])
-        transpose_x(1)
-        quantise_x(1)
-        bias_term(0, 0)
-        transpose_x(2)
-        transpose_x(3)
-        quantise_x(2)
-        bias_term(0, 1)
-        bias_term(0, 2)
-        quantise_x(3)
-        spread_biases(2, ("scalar", "scalar"))
-        bias_term(0, 3)
-        sort_pair(0)
+        spread_bias(1, "vector")
         for m in range(X_TILES):
-            base(0, m)
-        spread_biases(3, ("vector", "scalar"))
+            transpose_x(m)
+            if m + 2 < CHUNKS:
+                spread_bias(m + 2, "scalar")
+            quantise_x(m)
+        load_weight(3)
+        for i in range(QUAD):
+            sort_words(X_TILES + i, "scalar" if i < QUAD - 1 else "vector")
+            base(0, i)
 
         later_bases = [(c, m) for c in range(1, CHUNKS) for m in range(X_TILES)]
-        bases_in_round = [2, 1, 1, 1, 1, 1, 1, 2]
-        for h in range(PAIRS):
-            transpose_pair(h)
-            if h + 1 < PAIRS:
-                sort_pair(h + 1)
-            if h % 2 == 0 and h // 2 + 1 < CHUNKS:
+        bases_in_phase = [6, 3, 3, 0]
+        for c in range(CHUNKS):
+            transpose_quad(c)
+            if c + 1 < CHUNKS:
+                for i in range(QUAD):
+                    sort_words(X_TILES + QUAD * (c + 1) + i, "scalar")
+            products = [(perturbation, c - 1, m) for m in range(X_TILES)] if c > 0 else []
+            first = sum(bases_in_phase[:c])
+            products += [(base, cc, m) for cc, m in later_bases[first:first + bases_in_phase[c]]]
+            if c == CHUNKS - 1:
+                products += [(perturbation, c, m) for m in range(X_TILES)]
+            between = [(quantise_quad, c, 0), (quantise_quad, c, 1)]
+            if c == 0:
+                between += [(prev_bias_term, c, m) for m in range(X_TILES)]
+            else:
                 for m in range(X_TILES):
-                    bias_term(h // 2 + 1, m)
-            quantise_pair(h)
-            if h > 0:
-                perturbation(h - 1)
-            first = sum(bases_in_round[:h])
-            for c, m in later_bases[first:first + bases_in_round[h]]:
-                base(c, m)
-        perturbation(PAIRS - 1)
-        for c, m in later_bases[sum(bases_in_round):]:
-            base(c, m)
+                    prev_bias_term(c, m)
+                between = [None] + between
+            for i, (product_of, cc, m) in enumerate(products):
+                if i < len(between) and between[i] is not None:
+                    between[i][0](between[i][1], between[i][2])
+                product_of(cc, m)

@@ -89,6 +89,10 @@ def tile_optimizedlinear_kernel(
                 in_=weight_words[:, :, 2 * CHUNK * c:2 * CHUNK * (c + 1)].rearrange("g p b -> p g b").bitcast(I32),
             )
 
+        def load_prev_bias(c):
+            columns = slice(CHUNK * c, CHUNK * (c + 1))
+            nc.sync.dma_start(out=prev_bias_all[:, columns], in_=prev_bias_grad[columns].partition_broadcast(P))
+
         def strided_words(a):
             return raw[a][:].bitcast(F32).rearrange("r (g p u) -> r g u p", g=PASSES, u=2)
 
@@ -120,7 +124,7 @@ def tile_optimizedlinear_kernel(
 
         def transpose_quad(c):
             words = g_grouped[:].bitcast(F32)
-            if c == 0:
+            if c < 2:
                 order = [(i, half) for i in range(QUAD) for half in range(2)]
             else:
                 order = [(i, half) for half in range(2) for i in range(QUAD)]
@@ -185,31 +189,32 @@ def tile_optimizedlinear_kernel(
         for c in range(CHUNKS):
             nc.vector.memset(w_scales[c][:].bitcast(I32), 0)
 
+        load_rows(0)
         nc.sync.dma_start(out=bias_rows[0:1, :], in_=bias.unsqueeze(0))
         nc.sync.dma_start(out=lr_rows[0:X_TILES, :], in_=lr_samples.rearrange("(m p) -> m p", p=P))
-        for m in range(X_TILES):
+        for m in range(1, X_TILES):
             load_rows(m)
         load_weight(0)
         for i in range(QUAD):
             load_rows(X_TILES + i)
         load_weight(1)
-        nc.sync.dma_start(out=prev_bias_all[:], in_=prev_bias_grad.partition_broadcast(P))
+        load_prev_bias(0)
         load_rows(X_TILES + QUAD)
         load_rows(X_TILES + QUAD + 1)
         load_weight(2)
 
         nc.vector.tensor_scalar(out=neg_lr_rows[:], in0=lr_rows[:], scalar1=-1.0, scalar2=None, op0=MULT)
-        spread_bias(0, "scalar")
+        for m in range(X_TILES):
+            transpose_x(m)
+            spread_bias(m, "scalar")
+            quantise_x(m)
         lr_bank = banks.tile([P, 2, 2, P], F32, name="bank")
         nc.tensor.transpose(lr_bank[:, 0, 0, :], neg_lr_rows[:], identity[:])
         nc.vector.tensor_copy(out=neg_lr[:], in_=lr_bank[:, 0, 0, 0:X_TILES])
-        spread_bias(1, "vector")
-        for m in range(X_TILES):
-            transpose_x(m)
-            if m + 2 < CHUNKS:
-                spread_bias(m + 2, "scalar")
-            quantise_x(m)
+        load_prev_bias(1)
         load_weight(3)
+        load_prev_bias(2)
+        load_prev_bias(3)
         for i in range(QUAD):
             sort_words(X_TILES + i, "scalar" if i < QUAD - 1 else "vector")
             base(0, i)

@@ -77,13 +77,15 @@ def tile_optimizedlinear_kernel(
             if a + RAW_SLOTS < ROW_TILES:
                 load_rows(a + RAW_SLOTS)
 
-        def load_weight(c):
+        def load_weight_scales(c):
             rows = weight_scales.rearrange("g q n -> q g n")
             for r in range(4):
                 nc.sync.dma_start(
                     out=w_scales[c][r:P:32, :, :].bitcast(I32),
                     in_=rows[r:16:4, :, CHUNK * c:CHUNK * (c + 1)].bitcast(I32),
                 )
+
+        def load_weight_words(c):
             nc.sync.dma_start(
                 out=w_words[c][:].bitcast(I32),
                 in_=weight_words[:, :, 2 * CHUNK * c:2 * CHUNK * (c + 1)].rearrange("g p b -> p g b").bitcast(I32),
@@ -146,11 +148,10 @@ def tile_optimizedlinear_kernel(
             nc.tensor.matmul(out=bank[:], lhsT=first_row[:], rhs=bias_rows[:, columns], start=True, stop=True)
             copy(engine, bias_all[:, columns], bank[:])
 
-        def product(m, rhs, rhs_scale):
-            bank = banks.tile([P, CHUNK], F32, name="bank")
+        def product(acc, m, rhs, rhs_scale):
             for g in range(PASSES):
                 nc.tensor.matmul_mx(
-                    out=bank[:],
+                    out=acc,
                     lhsT=x_codes[m][:, g, :].bitcast(FP8X4),
                     lhsT_scale=x_scales[m][:, g, :],
                     rhs=rhs[g],
@@ -158,11 +159,12 @@ def tile_optimizedlinear_kernel(
                     start=(g == 0),
                     stop=(g == PASSES - 1),
                 )
-            return bank
 
         def base(c, m):
-            bank = product(
-                m, [w_words[c][:, g, :].bitcast(FP4X4) for g in range(PASSES)], [w_scales[c][:, g, :] for g in range(PASSES)]
+            bank = banks.tile([P, CHUNK], F32, name="bank")
+            product(
+                bank[:], m,
+                [w_words[c][:, g, :].bitcast(FP4X4) for g in range(PASSES)], [w_scales[c][:, g, :] for g in range(PASSES)],
             )
             nc.vector.tensor_tensor(out=o[m][c][:], in0=bank[:], in1=bias_all[:, CHUNK * c:CHUNK * (c + 1)], op=ADD)
 
@@ -173,35 +175,51 @@ def tile_optimizedlinear_kernel(
             )
 
         def perturbation(c, m):
-            bank = product(
-                m, [g_codes[c][:, g, :].bitcast(FP8X4) for g in range(PASSES)], [g_scales[c][:, g, :] for g in range(PASSES)]
-            )
-            nc.vector.scalar_tensor_tensor(
-                out=o[m][c][:], in0=bank[:], scalar=neg_lr[:, m:m + 1], in1=o[m][c][:], op0=MULT, op1=ADD,
-            )
-            nc.sync.dma_start(out=out[P * m:P * (m + 1), CHUNK * c:CHUNK * (c + 1)], in_=o[m][c][:])
+            width = CHUNK // 2 if (c, m) == (CHUNKS - 1, X_TILES - 1) else CHUNK
+            for first in range(0, CHUNK, width):
+                columns = slice(first, first + width)
+                bank = banks.tile([P, width], F32, name="bank")
+                product(
+                    bank[:], m,
+                    [g_codes[c][:, g, columns].bitcast(FP8X4) for g in range(PASSES)],
+                    [g_scales[c][:, g, columns] for g in range(PASSES)],
+                )
+                nc.vector.scalar_tensor_tensor(
+                    out=o[m][c][:, columns], in0=bank[:], scalar=neg_lr[:, m:m + 1], in1=o[m][c][:, columns],
+                    op0=MULT, op1=ADD,
+                )
+                nc.sync.dma_start(
+                    out=out[P * m:P * (m + 1), CHUNK * c + first:CHUNK * c + first + width], in_=o[m][c][:, columns]
+                )
 
         make_identity(nc, identity[:])
         nc.vector.memset(bias_rows[:].bitcast(I32), 0)
         nc.vector.memset(lr_rows[:], 0.0)
+        nc.vector.memset(w_scales[0][:].bitcast(I32), 0)
         nc.vector.memset(first_row[:], 0.0)
         nc.vector.memset(first_row[0:1, :], 1.0)
-        for c in range(CHUNKS):
+        for c in range(1, CHUNKS):
             nc.vector.memset(w_scales[c][:].bitcast(I32), 0)
 
         load_rows(0)
         nc.sync.dma_start(out=bias_rows[0:1, :], in_=bias.unsqueeze(0))
         nc.sync.dma_start(out=lr_rows[0:X_TILES, :], in_=lr_samples.rearrange("(m p) -> m p", p=P))
-        for m in range(1, X_TILES):
-            load_rows(m)
-        load_weight(0)
-        for i in range(QUAD):
-            load_rows(X_TILES + i)
-        load_weight(1)
+        load_rows(1)
+        load_weight_scales(0)
+        load_rows(2)
+        load_rows(3)
+        load_weight_words(0)
+        load_rows(X_TILES)
+        load_rows(X_TILES + 1)
+        load_weight_scales(1)
+        load_rows(X_TILES + 2)
+        load_rows(X_TILES + 3)
+        load_weight_words(1)
         load_prev_bias(0)
+        load_weight_scales(2)
         load_rows(X_TILES + QUAD)
         load_rows(X_TILES + QUAD + 1)
-        load_weight(2)
+        load_weight_words(2)
 
         nc.vector.tensor_scalar(out=neg_lr_rows[:], in0=lr_rows[:], scalar1=-1.0, scalar2=None, op0=MULT)
         for m in range(X_TILES):
@@ -212,7 +230,8 @@ def tile_optimizedlinear_kernel(
         nc.tensor.transpose(lr_bank[:, 0, 0, :], neg_lr_rows[:], identity[:])
         nc.vector.tensor_copy(out=neg_lr[:], in_=lr_bank[:, 0, 0, 0:X_TILES])
         load_prev_bias(1)
-        load_weight(3)
+        load_weight_scales(3)
+        load_weight_words(3)
         load_prev_bias(2)
         load_prev_bias(3)
         for i in range(QUAD):

from contextlib import ExitStack

import concourse.mybir as mybir
from concourse.masks import make_identity

F32 = mybir.dt.float32
BF16 = mybir.dt.bfloat16
I32 = mybir.dt.int32
U32 = mybir.dt.uint32
U8 = mybir.dt.uint8
FP8X4 = mybir.dt.float8_e4m3fn_x4
FP4X4 = mybir.dt.float4_e2m1fn_x4
MULT = mybir.AluOpType.mult
ADD = mybir.AluOpType.add

P = 128
B, IN, OUT = 512, 2048, 2048
PASSES = IN // 512
X_TILES = B // P
G_TILES = OUT // P
ROW_TILES = X_TILES + G_TILES
CHUNK = 512
CHUNKS = OUT // CHUNK
QUAD = CHUNK // P
RAW_SLOTS = 10
SORTED_SLOTS = 2 * QUAD
FLOPS = 2 * 2 * B * IN * OUT


def tile_optimizedlinear_kernel(
    tc, input_data, weight_words, weight_scales, bias, prev_grad, prev_bias_grad, lr_samples, out
):
    nc = tc.nc
    with ExitStack() as ctx:
        keep = ctx.enter_context(tc.tile_pool(name="keep", bufs=1))
        raw_pool = ctx.enter_context(tc.tile_pool(name="raw_pool", bufs=RAW_SLOTS))
        sorted_pool = ctx.enter_context(tc.tile_pool(name="sorted_pool", bufs=SORTED_SLOTS))
        grouped_pool = ctx.enter_context(tc.tile_pool(name="grouped_pool", bufs=2))
        banks = ctx.enter_context(tc.psum_pool(name="banks", bufs=8))
        ctx.enter_context(tc.manual_schedule())

        identity = keep.tile([P, P], F32, name="identity")
        lr_rows = keep.tile([P, P], BF16, name="lr_rows")
        neg_lr_rows = keep.tile([P, P], F32, name="neg_lr_rows")
        neg_lr = keep.tile([P, X_TILES], F32, name="neg_lr")
        bias_rows = keep.tile([P, OUT], BF16, name="bias_rows")
        first_row = keep.tile([P, P], BF16, name="first_row")
        bias_all = keep.tile([P, OUT], BF16, name="bias_all")
        prev_bias_all = keep.tile([P, OUT], BF16, name="prev_bias_all")
        w_words = [keep.tile([P, PASSES, 2 * CHUNK], U8, name="w_words%d" % c, align_bytes=64) for c in range(CHUNKS)]
        w_scales = [keep.tile([P, PASSES, CHUNK], U8, name="w_scales%d" % c, align_bytes=64) for c in range(CHUNKS)]
        x_codes = [keep.tile([P, PASSES, P], U32, name="x_codes%d" % m, align_bytes=64) for m in range(X_TILES)]
        x_scales = [keep.tile([P, PASSES, P], U8, name="x_scales%d" % m, align_bytes=64) for m in range(X_TILES)]
        g_codes = [keep.tile([P, PASSES, CHUNK], U32, name="g_codes%d" % c, align_bytes=64) for c in range(CHUNKS)]
        g_scales = [keep.tile([P, PASSES, CHUNK], U8, name="g_scales%d" % c, align_bytes=64) for c in range(CHUNKS)]
        g_grouped = keep.tile([P, PASSES, CHUNK, 4], BF16, name="g_grouped", align_bytes=64)
        o = [[keep.tile([P, CHUNK], F32, name="o%d_%d" % (m, c)) for c in range(CHUNKS)] for m in range(X_TILES)]
        raw = {}
        sorted_words = {}
        x_grouped = {}

        def copy(engine, dst, src):
            if engine == "vector":
                nc.vector.tensor_copy(out=dst, in_=src)
            else:
                nc.scalar.copy(out=dst, in_=src)

        def load_rows(a):
            if a < X_TILES:
                rows = input_data[P * a:P * (a + 1), :]
            else:
                rows = prev_grad[P * (a - X_TILES):P * (a - X_TILES + 1), :]
            raw[a] = raw_pool.tile([P, IN], BF16, name="raw")
            nc.sync.dma_start(out=raw[a][:], in_=rows)

        def slot_free(a):
            if a + RAW_SLOTS < ROW_TILES:
                load_rows(a + RAW_SLOTS)

        def load_weight_scales(c):
            rows = weight_scales.rearrange("g q n -> q g n")
            for r in range(4):
                nc.sync.dma_start(
                    out=w_scales[c][r:P:32, :, :].bitcast(I32),
                    in_=rows[r:16:4, :, CHUNK * c:CHUNK * (c + 1)].bitcast(I32),
                )

        def load_weight_words(c):
            nc.sync.dma_start(
                out=w_words[c][:].bitcast(I32),
                in_=weight_words[:, :, 2 * CHUNK * c:2 * CHUNK * (c + 1)].rearrange("g p b -> p g b").bitcast(I32),
            )

        def load_prev_bias(c):
            columns = slice(CHUNK * c, CHUNK * (c + 1))
            nc.sync.dma_start(out=prev_bias_all[:, columns], in_=prev_bias_grad[columns].partition_broadcast(P))

        def strided_words(a):
            return raw[a][:].bitcast(F32).rearrange("r (g p u) -> r g u p", g=PASSES, u=2)

        def sort_words(a, engine):
            sorted_words[a] = sorted_pool.tile([P, PASSES, 2, P], F32, name="sorted_words")
            copy(engine, sorted_words[a][:], strided_words(a))
            slot_free(a)

        def transpose_half(a, half, grouped_words, rows, engine):
            words = sorted_words[a] if a in sorted_words else strided_words(a)
            bank = banks.tile([P, 2, 2, P], F32, name="bank")
            for g in range(2):
                for u in range(2):
                    nc.tensor.transpose(bank[:, g, u, :], words[:, 2 * half + g, u, :], identity[:])
            copy(engine, grouped_words[:, 2 * half:2 * half + 2, rows, :], bank[:].rearrange("p g u r -> p g r u"))

        def transpose_x(m):
            x_grouped[m] = grouped_pool.tile([P, PASSES, P, 4], BF16, name="x_grouped", align_bytes=64)
            transpose_half(m, 0, x_grouped[m][:].bitcast(F32), slice(0, P), "scalar")
            transpose_half(m, 1, x_grouped[m][:].bitcast(F32), slice(0, P), "vector")
            slot_free(m)

        def quantise_x(m):
            nc.vector.quantize_mx(
                out=x_codes[m][:].rearrange("p g r -> p (g r)").bitcast(FP8X4),
                scales=x_scales[m][:].rearrange("p g r -> p (g r)"),
                in_=x_grouped[m][:].rearrange("p g r t -> p (g r t)"),
            )

        def transpose_quad(c):
            words = g_grouped[:].bitcast(F32)
            if c < 2:
                order = [(i, half) for i in range(QUAD) for half in range(2)]
            else:
                order = [(i, half) for half in range(2) for i in range(QUAD)]
            for i, half in order:
                engine = "vector" if c == 0 and half == 1 else "scalar"
                transpose_half(X_TILES + QUAD * c + i, half, words, slice(P * i, P * (i + 1)), engine)

        def quantise_quad(c, half):
            passes = slice(2 * half, 2 * half + 2)
            nc.vector.quantize_mx(
                out=g_codes[c][:, passes, :].rearrange("p g r -> p (g r)").bitcast(FP8X4),
                scales=g_scales[c][:, passes, :].rearrange("p g r -> p (g r)"),
                in_=g_grouped[:, passes, :, :].rearrange("p g r t -> p (g r t)"),
            )

        def spread_bias(c, engine):
            columns = slice(CHUNK * c, CHUNK * (c + 1))
            bank = banks.tile([P, CHUNK], F32, name="bank")
            nc.tensor.matmul(out=bank[:], lhsT=first_row[:], rhs=bias_rows[:, columns], start=True, stop=True)
            copy(engine, bias_all[:, columns], bank[:])

        def product(acc, m, rhs, rhs_scale):
            for g in range(PASSES):
                nc.tensor.matmul_mx(
                    out=acc,
                    lhsT=x_codes[m][:, g, :].bitcast(FP8X4),
                    lhsT_scale=x_scales[m][:, g, :],
                    rhs=rhs[g],
                    rhs_scale=rhs_scale[g],
                    start=(g == 0),
                    stop=(g == PASSES - 1),
                )

        def base(c, m):
            bank = banks.tile([P, CHUNK], F32, name="bank")
            product(
                bank[:], m,
                [w_words[c][:, g, :].bitcast(FP4X4) for g in range(PASSES)], [w_scales[c][:, g, :] for g in range(PASSES)],
            )
            nc.vector.tensor_tensor(out=o[m][c][:], in0=bank[:], in1=bias_all[:, CHUNK * c:CHUNK * (c + 1)], op=ADD)

        def prev_bias_term(c, m):
            nc.vector.scalar_tensor_tensor(
                out=o[m][c][:], in0=prev_bias_all[:, CHUNK * c:CHUNK * (c + 1)], scalar=neg_lr[:, m:m + 1], in1=o[m][c][:],
                op0=MULT, op1=ADD,
            )

        def perturbation(c, m):
            width = CHUNK // 2 if (c, m) == (CHUNKS - 1, X_TILES - 1) else CHUNK
            for first in range(0, CHUNK, width):
                columns = slice(first, first + width)
                bank = banks.tile([P, width], F32, name="bank")
                product(
                    bank[:], m,
                    [g_codes[c][:, g, columns].bitcast(FP8X4) for g in range(PASSES)],
                    [g_scales[c][:, g, columns] for g in range(PASSES)],
                )
                nc.vector.scalar_tensor_tensor(
                    out=o[m][c][:, columns], in0=bank[:], scalar=neg_lr[:, m:m + 1], in1=o[m][c][:, columns],
                    op0=MULT, op1=ADD,
                )
                nc.sync.dma_start(
                    out=out[P * m:P * (m + 1), CHUNK * c + first:CHUNK * c + first + width], in_=o[m][c][:, columns]
                )

        make_identity(nc, identity[:])
        nc.vector.memset(bias_rows[:].bitcast(I32), 0)
        nc.vector.memset(lr_rows[:], 0.0)
        nc.vector.memset(w_scales[0][:].bitcast(I32), 0)
        nc.vector.memset(first_row[:], 0.0)
        nc.vector.memset(first_row[0:1, :], 1.0)
        for c in range(1, CHUNKS):
            nc.vector.memset(w_scales[c][:].bitcast(I32), 0)

        load_rows(0)
        nc.sync.dma_start(out=bias_rows[0:1, :], in_=bias.unsqueeze(0))
        nc.sync.dma_start(out=lr_rows[0:X_TILES, :], in_=lr_samples.rearrange("(m p) -> m p", p=P))
        load_rows(1)
        load_weight_scales(0)
        load_rows(2)
        load_rows(3)
        load_weight_words(0)
        load_rows(X_TILES)
        load_rows(X_TILES + 1)
        load_weight_scales(1)
        load_rows(X_TILES + 2)
        load_rows(X_TILES + 3)
        load_weight_words(1)
        load_prev_bias(0)
        load_weight_scales(2)
        load_rows(X_TILES + QUAD)
        load_rows(X_TILES + QUAD + 1)
        load_weight_words(2)

        nc.vector.tensor_scalar(out=neg_lr_rows[:], in0=lr_rows[:], scalar1=-1.0, scalar2=None, op0=MULT)
        for m in range(X_TILES):
            transpose_x(m)
            spread_bias(m, "scalar")
            quantise_x(m)
        lr_bank = banks.tile([P, 2, 2, P], F32, name="bank")
        nc.tensor.transpose(lr_bank[:, 0, 0, :], neg_lr_rows[:], identity[:])
        nc.vector.tensor_copy(out=neg_lr[:], in_=lr_bank[:, 0, 0, 0:X_TILES])
        load_prev_bias(1)
        load_weight_scales(3)
        load_weight_words(3)
        load_prev_bias(2)
        load_prev_bias(3)
        for i in range(QUAD):
            sort_words(X_TILES + i, "scalar" if i < QUAD - 1 else "vector")
            base(0, i)

        later_bases = [(c, m) for c in range(1, CHUNKS) for m in range(X_TILES)]
        bases_in_phase = [6, 3, 3, 0]
        for c in range(CHUNKS):
            transpose_quad(c)
            if c + 1 < CHUNKS:
                for i in range(QUAD):
                    sort_words(X_TILES + QUAD * (c + 1) + i, "scalar")
            products = [(perturbation, c - 1, m) for m in range(X_TILES)] if c > 0 else []
            first = sum(bases_in_phase[:c])
            products += [(base, cc, m) for cc, m in later_bases[first:first + bases_in_phase[c]]]
            if c == CHUNKS - 1:
                products += [(perturbation, c, m) for m in range(X_TILES)]
            between = [(quantise_quad, c, 0), (quantise_quad, c, 1)]
            if c == 0:
                between += [(prev_bias_term, c, m) for m in range(X_TILES)]
            else:
                for m in range(X_TILES):
                    prev_bias_term(c, m)
                between = [None] + between
            for i, (product_of, cc, m) in enumerate(products):
                if i < len(between) and between[i] is not None:
                    between[i][0](between[i][1], between[i][2])
                product_of(cc, m)
